import numpy as np
import ml_dtypes


def mxq(x, axis, fmt="e4m3"):
    dtype, down = {"e4m3": (ml_dtypes.float8_e4m3fn, 7), "e5m2": (ml_dtypes.float8_e5m2, 14)}[fmt]
    v = np.moveaxis(np.asarray(x, np.float32).astype(ml_dtypes.bfloat16).astype(np.float64), axis, -1)
    blocks = v.reshape(v.shape[:-1] + (-1, 32))
    amax = np.abs(blocks).max(-1, keepdims=True)
    byte = np.maximum(np.where(amax > 0, np.frexp(amax)[1] - 1 + 127, 0) - down, 1)
    scale = np.exp2(byte - 127.0)
    codes = (blocks / scale).astype(np.float32).astype(dtype).astype(np.float64)
    return np.moveaxis((codes * scale).reshape(v.shape), -1, axis)


WIDE = False


def mx_kscale(k):
    if not WIDE:
        return np.ones(k)
    levels = np.array([10, -10, 5, -5, 0])
    a = np.random.permutation(np.resize(levels, k // 512 * 4)).reshape(k // 512, 4)
    idx = np.arange(k)
    return np.exp2(a[idx // 512, idx % 128 // 32])


BF16 = ml_dtypes.bfloat16


def bf(x):
    return np.asarray(x, np.float32).astype(BF16)


def f64(x):
    return np.asarray(x).astype(np.float64)


E2M1 = np.array([0.0, 0.5, 1.0, 1.5, 2.0, 3.0, 4.0, 6.0, -0.0, -0.5, -1.0, -1.5, -2.0, -3.0, -4.0, -6.0])


def pack_weight(w, fmt):
    k, n = w.shape
    w = f64(bf(w)).reshape(k // 32, 32, n)
    amax = np.abs(w).max(1)
    if fmt == "e4m3":
        byte = np.frexp(amax)[1] - 1 + 127 - 7
    else:
        mant, ex = np.frexp(amax / 6.0)
        byte = np.where(mant > 0.5, ex, ex - 1) + 127
    byte = np.clip(np.where(amax > 0, byte, 1), 1, 254)
    scaled = (w * np.exp2(127.0 - byte)[:, None, :]).reshape(k, n).astype(np.float32)
    by_word = np.ascontiguousarray(scaled.reshape(k // 512, 128, 4, n).transpose(0, 1, 3, 2))
    if fmt == "e4m3":
        words = by_word.astype(ml_dtypes.float8_e4m3fn).view(np.uint8)
    else:
        c = by_word.astype(ml_dtypes.float4_e2m1fn).view(np.uint8) & 0xF
        words = c[..., 0::2] | (c[..., 1::2] << 4)
    return np.ascontiguousarray(words), np.ascontiguousarray(byte.astype(np.uint8).reshape(k // 512, 16, n))


def unpack_weight(words, scales, fmt):
    g, p, n, _ = words.shape
    if fmt == "e4m3":
        vals = np.ascontiguousarray(words).view(ml_dtypes.float8_e4m3fn).astype(np.float64)
    else:
        nib = np.empty((g, p, n, 4), np.uint8)
        nib[..., 0::2] = words & 0xF
        nib[..., 1::2] = words >> 4
        vals = E2M1[nib]
    vals = vals * np.repeat(np.exp2(scales.astype(np.float64) - 127.0), 8, axis=1)[..., None]
    return vals.transpose(0, 1, 3, 2).reshape(g * 512, n)

def pack4(w):
    words, scales = pack_weight(w, "e2m1")
    return words.reshape(words.shape[0], 128, -1), scales


def unpack4(words, scales):
    return unpack_weight(words.reshape(words.shape[0], 128, -1, 2), scales, "e2m1")


G1, G2, B, DIM, K, N = 8, 8, 32, 2, 512, 256


def sigmoid(v):
    return 1.0 / (1.0 + np.exp(-v))


def setup_inputs():
    s = mx_kscale(K)
    a = 1.5 / np.sqrt(K)
    r = np.random.standard_normal
    x = bf(r((G1, G2, B, K)) * s)
    wf = bf(r((DIM, K, N)) * a)
    uf = bf(r((DIM, DIM, N)) * 0.5)
    biasf = bf(r((DIM, N)) * 0.5)
    wi = bf(r((K, N)) * a)
    ui = bf(r((DIM, N)) * 0.5)
    biasi = bf(r(N) * 0.5)
    wo_words, wo_scales = pack4(r((K, N)) * a / s[:, None])
    uo = bf(r((DIM, N)) * 0.5)
    biaso = bf(r(N) * 0.5)
    wc_words, wc_scales = pack4(r((K, N)) * a / s[:, None])
    uc = bf(r((DIM, N)) * 0.5)
    biasc = bf(r(N) * 0.5)
    return {
        "x": x,
        "wf": wf,
        "uf": uf,
        "biasf": biasf,
        "wi": wi,
        "ui": ui,
        "biasi": biasi,
        "wo_words": wo_words,
        "wo_scales": wo_scales,
        "uo": uo,
        "biaso": biaso,
        "wc_words": wc_words,
        "wc_scales": wc_scales,
        "uc": uc,
        "biasc": biasc,
    }


def reference(x, wf, uf, biasf, wi, ui, biasi, wo_words, wo_scales, uo, biaso, wc_words, wc_scales, uc, biasc):
    xq = mxq(f64(x), 3, "e4m3")
    o = sigmoid((xq @ unpack4(wo_words, wo_scales)) + f64(biaso))
    c = sigmoid((xq @ unpack4(wc_words, wc_scales)) + f64(biasc))
    return o * np.tanh(c)

@@ -1,0 +1,184 @@
+from contextlib import ExitStack
+
+import concourse.mybir as mybir
+from concourse.masks import make_identity
+
+F32 = mybir.dt.float32
+BF16 = mybir.dt.bfloat16
+I32 = mybir.dt.int32
+U8 = mybir.dt.uint8
+U32 = mybir.dt.uint32
+FP8X4 = mybir.dt.float8_e4m3fn_x4
+FP4X4 = mybir.dt.float4_e2m1fn_x4
+SIGMOID = mybir.ActivationFunctionType.Sigmoid
+TANH = mybir.ActivationFunctionType.Tanh
+MULT = mybir.AluOpType.mult
+
+P = 128
+ROWS = 8 * 8 * 32
+K = 512
+FEATURES = 256
+ROW_TILES = ROWS // P
+CHUNK_TILES = 2
+CHUNKS = ROW_TILES // CHUNK_TILES
+CHUNK_ROWS = CHUNK_TILES * P
+HALVES = FEATURES // P
+GATES = 2
+WORDS = K // 2
+QUADRANTS = 4
+
+GATE_LAG = 1
+STORE_LAG = 4
+
+FLOPS = 2 * ROWS * K * GATES * FEATURES
+BYTES = ROWS * K * 2 + GATES * (K * FEATURES // 2 + K // 32 * FEATURES + FEATURES * 2) + ROWS * FEATURES * 4
+
+
+def tile_mdlstm_kernel(
+    tc, x, wf, uf, biasf, wi, ui, biasi, wo_words, wo_scales, uo, biaso, wc_words, wc_scales, uc, biasc, out
+):
+    nc = tc.nc
+    x_rows = x.flatten_outer_dims().rearrange("(p t) k -> p t k", t=ROW_TILES)
+    out_rows = out.flatten_outer_dims().rearrange("(p t) n -> p t n", t=ROW_TILES)
+
+    with ExitStack() as ctx:
+        keep = ctx.enter_context(tc.tile_pool(name="keep", bufs=1))
+        stage = ctx.enter_context(tc.tile_pool(name="stage", bufs=2))
+        gates = ctx.enter_context(tc.tile_pool(name="gates", bufs=3))
+        products = ctx.enter_context(tc.tile_pool(name="products", bufs=STORE_LAG))
+        results = ctx.enter_context(tc.tile_pool(name="results", bufs=3))
+        psum = ctx.enter_context(tc.psum_pool(name="psum", bufs=2))
+        ctx.enter_context(tc.manual_schedule())
+
+        x_sb = keep.tile([P, ROW_TILES, K], BF16)
+        x_codes = keep.tile([P, ROWS], U32, align_bytes=64)
+        x_scales = keep.tile([P, ROWS], U8, align_bytes=64)
+        w_words = keep.tile([P, GATES * FEATURES * 2], U8, align_bytes=64)
+        w_scales = keep.tile([P, GATES * FEATURES], U8, align_bytes=64)
+        bias_rows = keep.tile([P, P], BF16)
+        bias_rows_f32 = keep.tile([P, P], F32)
+        bias_cols = keep.tile([P, GATES * HALVES], F32)
+        identity = keep.tile([P, P], F32)
+
+        def chunk_tiles(c):
+            return slice(c * CHUNK_TILES, (c + 1) * CHUNK_TILES)
+
+        def chunk_rows(c):
+            return slice(c * CHUNK_ROWS, (c + 1) * CHUNK_ROWS)
+
+        def load_x(c):
+            nc.sync.dma_start(out=x_sb[:, chunk_tiles(c), :], in_=x_rows[:, chunk_tiles(c), :])
+
+        def load_weight(gate, words, scales):
+            nc.sync.dma_start(
+                out=w_words[:, gate * FEATURES * 2 : (gate + 1) * FEATURES * 2].bitcast(I32),
+                in_=words.rearrange("g p b -> (g p) b").bitcast(I32),
+            )
+            scale_rows = scales.rearrange("g q n -> (g q) n")
+            for quadrant in range(QUADRANTS):
+                nc.sync.dma_start(
+                    out=w_scales[
+                        32 * quadrant : 32 * quadrant + 4, gate * FEATURES : (gate + 1) * FEATURES
+                    ].bitcast(I32),
+                    in_=scale_rows[4 * quadrant : 4 * quadrant + 4, :].bitcast(I32),
+                )
+
+        def transpose_x(c):
+            x_t = psum.tile([P, CHUNK_TILES, 2, P], F32, tag="x_t")
+            for i in range(CHUNK_TILES):
+                words = x_sb[:, c * CHUNK_TILES + i, :].bitcast(F32)
+                for parity in range(2):
+                    nc.tensor.transpose(x_t[:, i, parity, :], words[:, parity:WORDS:2], identity[:])
+            grouped = stage.tile([P, CHUNK_ROWS * 4], BF16, align_bytes=64)
+            nc.vector.tensor_copy(
+                out=grouped[:].bitcast(F32).rearrange("p (i r w) -> p i r w", i=CHUNK_TILES, w=2),
+                in_=x_t[:].rearrange("p i w r -> p i r w"),
+            )
+            return grouped
+
+        def quantise_x(c, grouped):
+            nc.vector.quantize_mx(
+                out=x_codes[:, chunk_rows(c)].bitcast(FP8X4), scales=x_scales[:, chunk_rows(c)], in_=grouped[:]
+            )
+
+        def multiply(c, gate, acc):
+            for half in range(HALVES):
+                block = gate * HALVES + half
+                nc.tensor.matmul_mx(
+                    out=acc[:, half, :],
+                    lhsT=w_words[:, block * P * 2 : (block + 1) * P * 2].bitcast(FP4X4),
+                    lhsT_scale=w_scales[:, block * P : (block + 1) * P],
+                    rhs=x_codes[:, chunk_rows(c)].bitcast(FP8X4),
+                    rhs_scale=x_scales[:, chunk_rows(c)],
+                    start=True,
+                    stop=True,
+                )
+
+        def sigmoid(gate, half, acc, result):
+            block = gate * HALVES + half
+            nc.scalar.activation(
+                out=result[:, half, :], in_=acc[:, half, :], func=SIGMOID, bias=bias_cols[:, block : block + 1]
+            )
+
+        def cell(c):
+            o_acc = psum.tile([P, HALVES, CHUNK_ROWS], F32, tag="o_acc")
+            c_acc = psum.tile([P, HALVES, CHUNK_ROWS], F32, tag="c_acc")
+            multiply(c, 1, c_acc)
+            multiply(c, 0, o_acc)
+            o_sig = gates.tile([P, HALVES, CHUNK_ROWS], F32)
+            c_sig = gates.tile([P, HALVES, CHUNK_ROWS], F32)
+            c_tanh = gates.tile([P, HALVES, CHUNK_ROWS], F32)
+            product = products.tile([P, HALVES, CHUNK_ROWS], F32)
+            sigmoid(1, 0, c_acc, c_sig)
+            sigmoid(1, 1, c_acc, c_sig)
+            sigmoid(0, 0, o_acc, o_sig)
+            nc.scalar.activation(out=c_tanh[:], in_=c_sig[:], func=TANH)
+            sigmoid(0, 1, o_acc, o_sig)
+            for half in range(HALVES):
+                nc.gpsimd.tensor_tensor(
+                    out=product[:, half, :], in0=o_sig[:, half, :], in1=c_tanh[:, half, :], op=MULT
+                )
+            return product
+
+        def transpose_back(product):
+            out_t = psum.tile([P, CHUNK_TILES, FEATURES], F32, tag="out_t")
+            for i in range(CHUNK_TILES):
+                for half in range(HALVES):
+                    nc.tensor.transpose(
+                        out_t[:, i, half * P : (half + 1) * P], product[:, half, i * P : (i + 1) * P], identity[:]
+                    )
+            return out_t
+
+        def store(c, out_t):
+            result = results.tile([P, CHUNK_TILES, FEATURES], F32)
+            nc.vector.tensor_copy(out=result[:], in_=out_t[:])
+            nc.sync.dma_start(out=out_rows[:, chunk_tiles(c), :], in_=result[:])
+
+        nc.vector.memset(w_scales[:].bitcast(I32), 0)
+        nc.vector.memset(bias_rows[:], 0.0)
+        make_identity(nc, identity[:])
+        nc.scalar.dma_start(out=bias_rows[0:HALVES, :], in_=biaso.rearrange("(h n) -> h n", h=HALVES))
+        nc.scalar.dma_start(out=bias_rows[HALVES : 2 * HALVES, :], in_=biasc.rearrange("(h n) -> h n", h=HALVES))
+        load_x(0)
+        load_x(1)
+        load_weight(1, wc_words, wc_scales)
+        load_weight(0, wo_words, wo_scales)
+        for c in range(2, CHUNKS):
+            load_x(c)
+
+        nc.vector.tensor_copy(out=bias_rows_f32[:], in_=bias_rows[:])
+        bias_t = psum.tile([P, P], F32, tag="x_t")
+        nc.tensor.transpose(bias_t[:], bias_rows_f32[:], identity[:])
+        nc.vector.tensor_copy(out=bias_cols[:], in_=bias_t[:, 0 : GATES * HALVES])
+
+        product_of = {}
+        for step in range(CHUNKS + STORE_LAG):
+            if step < CHUNKS:
+                grouped = transpose_x(step)
+            if step >= STORE_LAG:
+                out_t = transpose_back(product_of[step - STORE_LAG])
+                store(step - STORE_LAG, out_t)
+            if step < CHUNKS:
+                quantise_x(step, grouped)
+            if GATE_LAG <= step < CHUNKS + GATE_LAG:
+                product_of[step - GATE_LAG] = cell(step - GATE_LAG)

@@ -19,9 +19,13 @@ ROWS = 8 * 8 * 32
 K = 512
 FEATURES = 256
 ROW_TILES = ROWS // P
-CHUNK_TILES = 2
-CHUNKS = ROW_TILES // CHUNK_TILES
-CHUNK_ROWS = CHUNK_TILES * P
+FULL_CHUNK = 2
+FULL_ROWS = FULL_CHUNK * P
+EDGE_CHUNKS = 2
+CHUNK_SIZES = [1] * EDGE_CHUNKS + [FULL_CHUNK] * ((ROW_TILES - 2 * EDGE_CHUNKS) // FULL_CHUNK) + [1] * EDGE_CHUNKS
+CHUNKS = len(CHUNK_SIZES)
+FIRST_TILE = [sum(CHUNK_SIZES[:c]) for c in range(CHUNKS)]
+assert sum(CHUNK_SIZES) == ROW_TILES
 HALVES = FEATURES // P
 GATES = 2
 WORDS = K // 2
@@ -59,12 +63,13 @@ def tile_mdlstm_kernel(
         bias_rows_f32 = keep.tile([P, P], F32)
         bias_cols = keep.tile([P, GATES * HALVES], F32)
         identity = keep.tile([P, P], F32)
+        table_warmer = keep.tile([P, 2], F32)
 
         def chunk_tiles(c):
-            return slice(c * CHUNK_TILES, (c + 1) * CHUNK_TILES)
+            return slice(FIRST_TILE[c], FIRST_TILE[c] + CHUNK_SIZES[c])
 
         def chunk_rows(c):
-            return slice(c * CHUNK_ROWS, (c + 1) * CHUNK_ROWS)
+            return slice(FIRST_TILE[c] * P, (FIRST_TILE[c] + CHUNK_SIZES[c]) * P)
 
         def load_x(c):
             nc.sync.dma_start(out=x_sb[:, chunk_tiles(c), :], in_=x_rows[:, chunk_tiles(c), :])
@@ -84,28 +89,31 @@ def tile_mdlstm_kernel(
                 )
 
         def transpose_x(c):
-            x_t = psum.tile([P, CHUNK_TILES, 2, P], F32, tag="x_t")
-            for i in range(CHUNK_TILES):
-                words = x_sb[:, c * CHUNK_TILES + i, :].bitcast(F32)
+            tiles = CHUNK_SIZES[c]
+            x_t = psum.tile([P, FULL_CHUNK, 2, P], F32, tag="x_t")
+            for i in range(tiles):
+                words = x_sb[:, FIRST_TILE[c] + i, :].bitcast(F32)
                 for parity in range(2):
                     nc.tensor.transpose(x_t[:, i, parity, :], words[:, parity:WORDS:2], identity[:])
-            grouped = stage.tile([P, CHUNK_ROWS * 4], BF16, align_bytes=64)
+            grouped = stage.tile([P, FULL_ROWS * 4], BF16, align_bytes=64)
             nc.vector.tensor_copy(
-                out=grouped[:].bitcast(F32).rearrange("p (i r w) -> p i r w", i=CHUNK_TILES, w=2),
-                in_=x_t[:].rearrange("p i w r -> p i r w"),
+                out=grouped[:, : tiles * P * 4].bitcast(F32).rearrange("p (i r w) -> p i r w", i=tiles, w=2),
+                in_=x_t[:, :tiles].rearrange("p i w r -> p i r w"),
             )
             return grouped
 
         def quantise_x(c, grouped):
             nc.vector.quantize_mx(
-                out=x_codes[:, chunk_rows(c)].bitcast(FP8X4), scales=x_scales[:, chunk_rows(c)], in_=grouped[:]
+                out=x_codes[:, chunk_rows(c)].bitcast(FP8X4),
+                scales=x_scales[:, chunk_rows(c)],
+                in_=grouped[:, : CHUNK_SIZES[c] * P * 4],
             )
 
         def multiply(c, gate, acc):
             for half in range(HALVES):
                 block = gate * HALVES + half
                 nc.tensor.matmul_mx(
-                    out=acc[:, half, :],
+                    out=acc[:, half, : CHUNK_SIZES[c] * P],
                     lhsT=w_words[:, block * P * 2 : (block + 1) * P * 2].bitcast(FP4X4),
                     lhsT_scale=w_scales[:, block * P : (block + 1) * P],
                     rhs=x_codes[:, chunk_rows(c)].bitcast(FP8X4),
@@ -114,35 +122,39 @@ def tile_mdlstm_kernel(
                     stop=True,
                 )
 
-        def sigmoid(gate, half, acc, result):
+        def sigmoid(gate, half, rows, acc, result):
             block = gate * HALVES + half
             nc.scalar.activation(
-                out=result[:, half, :], in_=acc[:, half, :], func=SIGMOID, bias=bias_cols[:, block : block + 1]
+                out=result[:, half, :rows],
+                in_=acc[:, half, :rows],
+                func=SIGMOID,
+                bias=bias_cols[:, block : block + 1],
             )
 
         def cell(c):
-            o_acc = psum.tile([P, HALVES, CHUNK_ROWS], F32, tag="o_acc")
-            c_acc = psum.tile([P, HALVES, CHUNK_ROWS], F32, tag="c_acc")
+            rows = CHUNK_SIZES[c] * P
+            o_acc = psum.tile([P, HALVES, FULL_ROWS], F32, tag="o_acc")
+            c_acc = psum.tile([P, HALVES, FULL_ROWS], F32, tag="c_acc")
             multiply(c, 1, c_acc)
             multiply(c, 0, o_acc)
-            o_sig = gates.tile([P, HALVES, CHUNK_ROWS], F32)
-            c_sig = gates.tile([P, HALVES, CHUNK_ROWS], F32)
-            c_tanh = gates.tile([P, HALVES, CHUNK_ROWS], F32)
-            product = products.tile([P, HALVES, CHUNK_ROWS], F32)
-            sigmoid(1, 0, c_acc, c_sig)
-            sigmoid(1, 1, c_acc, c_sig)
-            sigmoid(0, 0, o_acc, o_sig)
-            nc.scalar.activation(out=c_tanh[:], in_=c_sig[:], func=TANH)
-            sigmoid(0, 1, o_acc, o_sig)
+            o_sig = gates.tile([P, HALVES, FULL_ROWS], F32)
+            c_sig = gates.tile([P, HALVES, FULL_ROWS], F32)
+            c_tanh = gates.tile([P, HALVES, FULL_ROWS], F32)
+            product = products.tile([P, HALVES, FULL_ROWS], F32)
             for half in range(HALVES):
+                sigmoid(1, half, rows, c_acc, c_sig)
+            for half in range(HALVES):
+                nc.scalar.activation(out=c_tanh[:, half, :rows], in_=c_sig[:, half, :rows], func=TANH)
+            for half in range(HALVES):
+                sigmoid(0, half, rows, o_acc, o_sig)
                 nc.gpsimd.tensor_tensor(
-                    out=product[:, half, :], in0=o_sig[:, half, :], in1=c_tanh[:, half, :], op=MULT
+                    out=product[:, half, :rows], in0=o_sig[:, half, :rows], in1=c_tanh[:, half, :rows], op=MULT
                 )
             return product
 
-        def transpose_back(product):
-            out_t = psum.tile([P, CHUNK_TILES, FEATURES], F32, tag="out_t")
-            for i in range(CHUNK_TILES):
+        def transpose_back(c, product):
+            out_t = psum.tile([P, FULL_CHUNK, FEATURES], F32, tag="out_t")
+            for i in range(CHUNK_SIZES[c]):
                 for half in range(HALVES):
                     nc.tensor.transpose(
                         out_t[:, i, half * P : (half + 1) * P], product[:, half, i * P : (i + 1) * P], identity[:]
@@ -150,20 +162,24 @@ def tile_mdlstm_kernel(
             return out_t
 
         def store(c, out_t):
-            result = results.tile([P, CHUNK_TILES, FEATURES], F32)
-            nc.vector.tensor_copy(out=result[:], in_=out_t[:])
-            nc.sync.dma_start(out=out_rows[:, chunk_tiles(c), :], in_=result[:])
+            tiles = CHUNK_SIZES[c]
+            result = results.tile([P, FULL_CHUNK, FEATURES], F32)
+            nc.vector.tensor_copy(out=result[:, :tiles, :], in_=out_t[:, :tiles, :])
+            nc.sync.dma_start(out=out_rows[:, chunk_tiles(c), :], in_=result[:, :tiles, :])
 
+        nc.vector.memset(table_warmer[:], 0.0)
         nc.vector.memset(w_scales[:].bitcast(I32), 0)
         nc.vector.memset(bias_rows[:], 0.0)
         make_identity(nc, identity[:])
         nc.scalar.dma_start(out=bias_rows[0:HALVES, :], in_=biaso.rearrange("(h n) -> h n", h=HALVES))
         nc.scalar.dma_start(out=bias_rows[HALVES : 2 * HALVES, :], in_=biasc.rearrange("(h n) -> h n", h=HALVES))
+        nc.scalar.activation(out=table_warmer[:, 1:2], in_=table_warmer[:, 0:1], func=SIGMOID)
         load_x(0)
         load_x(1)
         load_weight(1, wc_words, wc_scales)
+        load_x(2)
         load_weight(0, wo_words, wo_scales)
-        for c in range(2, CHUNKS):
+        for c in range(3, CHUNKS):
             load_x(c)
 
         nc.vector.tensor_copy(out=bias_rows_f32[:], in_=bias_rows[:])
@@ -176,7 +192,7 @@ def tile_mdlstm_kernel(
             if step < CHUNKS:
                 grouped = transpose_x(step)
             if step >= STORE_LAG:
-                out_t = transpose_back(product_of[step - STORE_LAG])
+                out_t = transpose_back(step - STORE_LAG, product_of[step - STORE_LAG])
                 store(step - STORE_LAG, out_t)
             if step < CHUNKS:
                 quantise_x(step, grouped)

@@ -13,26 +13,29 @@ FP4X4 = mybir.dt.float4_e2m1fn_x4
 SIGMOID = mybir.ActivationFunctionType.Sigmoid
 TANH = mybir.ActivationFunctionType.Tanh
 MULT = mybir.AluOpType.mult
+ADD = mybir.AluOpType.add
 
 P = 128
 ROWS = 8 * 8 * 32
 K = 512
 FEATURES = 256
 ROW_TILES = ROWS // P
-FULL_CHUNK = 2
-FULL_ROWS = FULL_CHUNK * P
-EDGE_CHUNKS = 2
-CHUNK_SIZES = [1] * EDGE_CHUNKS + [FULL_CHUNK] * ((ROW_TILES - 2 * EDGE_CHUNKS) // FULL_CHUNK) + [1] * EDGE_CHUNKS
-CHUNKS = len(CHUNK_SIZES)
-FIRST_TILE = [sum(CHUNK_SIZES[:c]) for c in range(CHUNKS)]
-assert sum(CHUNK_SIZES) == ROW_TILES
 HALVES = FEATURES // P
 GATES = 2
 WORDS = K // 2
 QUADRANTS = 4
+UNIT = 2
+BANK = 512
 
-GATE_LAG = 1
-STORE_LAG = 4
+W_CHUNKS = [1, 1, 2, 2, 2, 2, 2]
+X_GROUPS = [2, 1, 1]
+assert sum(W_CHUNKS) + sum(X_GROUPS) == ROW_TILES
+MAX_ROWS = max(W_CHUNKS) * P
+SCALAR_COPIES = 2
+X_UNITS = [1, 1, 2, 2, 2, 2, 2, 2, 2]
+assert sum(X_UNITS) == ROW_TILES
+BACK_LAG = 2
+PRODUCTS = 4
 
 FLOPS = 2 * ROWS * K * GATES * FEATURES
 BYTES = ROWS * K * 2 + GATES * (K * FEATURES // 2 + K // 32 * FEATURES + FEATURES * 2) + ROWS * FEATURES * 4
@@ -45,34 +48,44 @@ def tile_mdlstm_kernel(
     x_rows = x.flatten_outer_dims().rearrange("(p t) k -> p t k", t=ROW_TILES)
     out_rows = out.flatten_outer_dims().rearrange("(p t) n -> p t n", t=ROW_TILES)
 
+    chunks = []
+    first_tile = 0
+    for kind, sizes in (("W", W_CHUNKS), ("X", X_GROUPS)):
+        for size in sizes:
+            chunks.append((kind, first_tile, size))
+            first_tile += size
+    units = []
+    first_tile = 0
+    for size in X_UNITS:
+        units.append((first_tile, size))
+        first_tile += size
+    n_w = len(W_CHUNKS)
+
     with ExitStack() as ctx:
         keep = ctx.enter_context(tc.tile_pool(name="keep", bufs=1))
-        stage = ctx.enter_context(tc.tile_pool(name="stage", bufs=2))
+        stage = ctx.enter_context(tc.tile_pool(name="stage", bufs=3))
         gates = ctx.enter_context(tc.tile_pool(name="gates", bufs=3))
-        products = ctx.enter_context(tc.tile_pool(name="products", bufs=STORE_LAG))
-        results = ctx.enter_context(tc.tile_pool(name="results", bufs=3))
+        products = ctx.enter_context(tc.tile_pool(name="products", bufs=PRODUCTS))
         psum = ctx.enter_context(tc.psum_pool(name="psum", bufs=2))
+        acc_pool = ctx.enter_context(tc.psum_pool(name="acc_pool", bufs=4))
         ctx.enter_context(tc.manual_schedule())
 
         x_sb = keep.tile([P, ROW_TILES, K], BF16)
+        out_sb = keep.tile([P, ROW_TILES, FEATURES], F32)
         x_codes = keep.tile([P, ROWS], U32, align_bytes=64)
         x_scales = keep.tile([P, ROWS], U8, align_bytes=64)
         w_words = keep.tile([P, GATES * FEATURES * 2], U8, align_bytes=64)
         w_scales = keep.tile([P, GATES * FEATURES], U8, align_bytes=64)
-        bias_rows = keep.tile([P, P], BF16)
-        bias_rows_f32 = keep.tile([P, P], F32)
+        bias_row = keep.tile([P, GATES * FEATURES], BF16)
+        ones = keep.tile([P, P], BF16)
         bias_cols = keep.tile([P, GATES * HALVES], F32)
+        bias_wide = keep.tile([P, GATES * FEATURES], F32)
         identity = keep.tile([P, P], F32)
         table_warmer = keep.tile([P, 2], F32)
 
-        def chunk_tiles(c):
-            return slice(FIRST_TILE[c], FIRST_TILE[c] + CHUNK_SIZES[c])
-
-        def chunk_rows(c):
-            return slice(FIRST_TILE[c] * P, (FIRST_TILE[c] + CHUNK_SIZES[c]) * P)
-
-        def load_x(c):
-            nc.sync.dma_start(out=x_sb[:, chunk_tiles(c), :], in_=x_rows[:, chunk_tiles(c), :])
+        def load_x(u):
+            first, size = units[u]
+            nc.sync.dma_start(out=x_sb[:, first : first + size, :], in_=x_rows[:, first : first + size, :])
 
         def load_weight(gate, words, scales):
             nc.sync.dma_start(
@@ -88,113 +101,199 @@ def tile_mdlstm_kernel(
                     in_=scale_rows[4 * quadrant : 4 * quadrant + 4, :].bitcast(I32),
                 )
 
-        def transpose_x(c):
-            tiles = CHUNK_SIZES[c]
-            x_t = psum.tile([P, FULL_CHUNK, 2, P], F32, tag="x_t")
+        def transpose_x(u):
+            first, tiles = units[u]
+            x_t = psum.tile([P, UNIT, 2, P], F32, tag="x_t")
             for i in range(tiles):
-                words = x_sb[:, FIRST_TILE[c] + i, :].bitcast(F32)
+                words = x_sb[:, first + i, :].bitcast(F32)
                 for parity in range(2):
                     nc.tensor.transpose(x_t[:, i, parity, :], words[:, parity:WORDS:2], identity[:])
-            grouped = stage.tile([P, FULL_ROWS * 4], BF16, align_bytes=64)
-            nc.vector.tensor_copy(
-                out=grouped[:, : tiles * P * 4].bitcast(F32).rearrange("p (i r w) -> p i r w", i=tiles, w=2),
-                in_=x_t[:, :tiles].rearrange("p i w r -> p i r w"),
-            )
+            grouped = stage.tile([P, UNIT * P * 4], BF16, align_bytes=64)
+            target = grouped[:, : tiles * P * 4].bitcast(F32).rearrange("p (i r w) -> p i r w", i=tiles, w=2)
+            source = x_t[:, :tiles].rearrange("p i w r -> p i r w")
+            if u < SCALAR_COPIES:
+                nc.scalar.copy(out=target, in_=source)
+            else:
+                nc.vector.tensor_copy(out=target, in_=source)
             return grouped
 
-        def quantise_x(c, grouped):
+        def quantise_x(u, grouped):
+            first, tiles = units[u]
+            rows = slice(first * P, (first + tiles) * P)
             nc.vector.quantize_mx(
-                out=x_codes[:, chunk_rows(c)].bitcast(FP8X4),
-                scales=x_scales[:, chunk_rows(c)],
-                in_=grouped[:, : CHUNK_SIZES[c] * P * 4],
+                out=x_codes[:, rows].bitcast(FP8X4),
+                scales=x_scales[:, rows],
+                in_=grouped[:, : tiles * P * 4],
             )
 
-        def multiply(c, gate, acc):
-            for half in range(HALVES):
+        def multiply_w(j):
+            kind, first, tiles = chunks[j]
+            rows = tiles * P
+            cols = slice(first * P, first * P + rows)
+            views = {}
+            for gate in (1, 0):
+                halves = []
+                if tiles <= UNIT:
+                    bank = acc_pool.tile([P, HALVES, UNIT * P], F32, tag="acc")
+                    for half in range(HALVES):
+                        halves.append(bank[:, half, :rows])
+                else:
+                    for half in range(HALVES):
+                        bank = acc_pool.tile([P, BANK], F32, tag="acc")
+                        halves.append(bank[:, :rows])
+                for half in range(HALVES):
+                    block = gate * HALVES + half
+                    nc.tensor.matmul_mx(
+                        out=halves[half],
+                        lhsT=w_words[:, block * P * 2 : (block + 1) * P * 2].bitcast(FP4X4),
+                        lhsT_scale=w_scales[:, block * P : (block + 1) * P],
+                        rhs=x_codes[:, cols].bitcast(FP8X4),
+                        rhs_scale=x_scales[:, cols],
+                        start=True,
+                        stop=True,
+                    )
+                views[gate] = halves
+            return views
+
+        def cell_w(j, acc):
+            kind, first, tiles = chunks[j]
+            rows = tiles * P
+            o_sig = gates.tile([P, HALVES, MAX_ROWS], F32)
+            c_sig = gates.tile([P, HALVES, MAX_ROWS], F32)
+            c_tanh = gates.tile([P, HALVES, MAX_ROWS], F32)
+            product = products.tile([P, HALVES, MAX_ROWS], F32)
+
+            def sigmoid(gate, half, result):
                 block = gate * HALVES + half
-                nc.tensor.matmul_mx(
-                    out=acc[:, half, : CHUNK_SIZES[c] * P],
-                    lhsT=w_words[:, block * P * 2 : (block + 1) * P * 2].bitcast(FP4X4),
-                    lhsT_scale=w_scales[:, block * P : (block + 1) * P],
-                    rhs=x_codes[:, chunk_rows(c)].bitcast(FP8X4),
-                    rhs_scale=x_scales[:, chunk_rows(c)],
-                    start=True,
-                    stop=True,
+                nc.scalar.activation(
+                    out=result[:, half, :rows],
+                    in_=acc[gate][half],
+                    func=SIGMOID,
+                    bias=bias_cols[:, block : block + 1],
                 )
 
-        def sigmoid(gate, half, rows, acc, result):
-            block = gate * HALVES + half
-            nc.scalar.activation(
-                out=result[:, half, :rows],
-                in_=acc[:, half, :rows],
-                func=SIGMOID,
-                bias=bias_cols[:, block : block + 1],
-            )
-
-        def cell(c):
-            rows = CHUNK_SIZES[c] * P
-            o_acc = psum.tile([P, HALVES, FULL_ROWS], F32, tag="o_acc")
-            c_acc = psum.tile([P, HALVES, FULL_ROWS], F32, tag="c_acc")
-            multiply(c, 1, c_acc)
-            multiply(c, 0, o_acc)
-            o_sig = gates.tile([P, HALVES, FULL_ROWS], F32)
-            c_sig = gates.tile([P, HALVES, FULL_ROWS], F32)
-            c_tanh = gates.tile([P, HALVES, FULL_ROWS], F32)
-            product = products.tile([P, HALVES, FULL_ROWS], F32)
-            for half in range(HALVES):
-                sigmoid(1, half, rows, c_acc, c_sig)
-            for half in range(HALVES):
-                nc.scalar.activation(out=c_tanh[:, half, :rows], in_=c_sig[:, half, :rows], func=TANH)
-            for half in range(HALVES):
-                sigmoid(0, half, rows, o_acc, o_sig)
+            def multiply(half):
                 nc.gpsimd.tensor_tensor(
                     out=product[:, half, :rows], in0=o_sig[:, half, :rows], in1=c_tanh[:, half, :rows], op=MULT
                 )
+
+            sigmoid(1, 0, c_sig)
+            sigmoid(1, 1, c_sig)
+            sigmoid(0, 0, o_sig)
+            nc.scalar.activation(out=c_tanh[:, :, :rows], in_=c_sig[:, :, :rows], func=TANH)
+            multiply(0)
+            sigmoid(0, 1, o_sig)
+            multiply(1)
             return product
 
-        def transpose_back(c, product):
-            out_t = psum.tile([P, FULL_CHUNK, FEATURES], F32, tag="out_t")
-            for i in range(CHUNK_SIZES[c]):
+        def back(j, product):
+            kind, first, tiles = chunks[j]
+            chunk_first = first
+            out_t = psum.tile([P, UNIT, FEATURES], F32, tag="out_t")
+            for i in range(tiles):
+                r0 = (first + i - chunk_first) * P
                 for half in range(HALVES):
                     nc.tensor.transpose(
-                        out_t[:, i, half * P : (half + 1) * P], product[:, half, i * P : (i + 1) * P], identity[:]
+                        out_t[:, i, half * P : (half + 1) * P], product[:, half, r0 : r0 + P], identity[:]
                     )
-            return out_t
+            nc.vector.tensor_copy(out=out_sb[:, first : first + tiles, :], in_=out_t[:, :tiles, :])
+            nc.sync.dma_start(out=out_rows[:, first : first + tiles, :], in_=out_sb[:, first : first + tiles, :])
 
-        def store(c, out_t):
-            tiles = CHUNK_SIZES[c]
-            result = results.tile([P, FULL_CHUNK, FEATURES], F32)
-            nc.vector.tensor_copy(out=result[:, :tiles, :], in_=out_t[:, :tiles, :])
-            nc.sync.dma_start(out=out_rows[:, chunk_tiles(c), :], in_=result[:, :tiles, :])
+        def prepare_x(j):
+            kind, first, tiles = chunks[j]
+            pre = gates.tile([P, UNIT, GATES * FEATURES], F32)
+            for i in range(tiles):
+                rows = slice((first + i) * P, (first + i + 1) * P)
+                acc = psum.tile([P, GATES * FEATURES], F32, tag="x_t")
+                nc.tensor.matmul_mx(
+                    out=acc[:],
+                    lhsT=x_codes[:, rows].bitcast(FP8X4),
+                    lhsT_scale=x_scales[:, rows],
+                    rhs=w_words[:].bitcast(FP4X4),
+                    rhs_scale=w_scales[:],
+                    start=True,
+                    stop=True,
+                )
+                nc.vector.tensor_tensor(out=pre[:, i, :], in0=acc[:], in1=bias_wide[:], op=ADD)
+            return pre
+
+        def cell_x(j, pre):
+            kind, first, tiles = chunks[j]
+            sig = gates.tile([P, UNIT, GATES * FEATURES], F32)
+            x_tanh = gates.tile([P, UNIT, FEATURES], F32)
+            nc.scalar.activation(out=sig[:, :tiles, FEATURES:], in_=pre[:, :tiles, FEATURES:], func=SIGMOID)
+            nc.scalar.activation(out=sig[:, :tiles, :FEATURES], in_=pre[:, :tiles, :FEATURES], func=SIGMOID)
+            nc.scalar.activation(out=x_tanh[:, :tiles, :], in_=sig[:, :tiles, FEATURES:], func=TANH)
+            nc.vector.tensor_tensor(
+                out=out_sb[:, first : first + tiles, :], in0=sig[:, :tiles, :FEATURES], in1=x_tanh[:, :tiles, :], op=MULT
+            )
+            nc.sync.dma_start(out=out_rows[:, first : first + tiles, :], in_=out_sb[:, first : first + tiles, :])
 
         nc.vector.memset(table_warmer[:], 0.0)
         nc.vector.memset(w_scales[:].bitcast(I32), 0)
-        nc.vector.memset(bias_rows[:], 0.0)
+        nc.vector.memset(bias_row[:], 0.0)
+        nc.vector.memset(ones[:], 1.0)
         make_identity(nc, identity[:])
-        nc.scalar.dma_start(out=bias_rows[0:HALVES, :], in_=biaso.rearrange("(h n) -> h n", h=HALVES))
-        nc.scalar.dma_start(out=bias_rows[HALVES : 2 * HALVES, :], in_=biasc.rearrange("(h n) -> h n", h=HALVES))
+        nc.scalar.dma_start(out=bias_row[0:1, 0:FEATURES], in_=biaso.rearrange("(a n) -> a n", a=1))
+        nc.scalar.dma_start(out=bias_row[0:1, FEATURES:], in_=biasc.rearrange("(a n) -> a n", a=1))
         nc.scalar.activation(out=table_warmer[:, 1:2], in_=table_warmer[:, 0:1], func=SIGMOID)
         load_x(0)
         load_x(1)
-        load_weight(1, wc_words, wc_scales)
         load_x(2)
+        load_weight(1, wc_words, wc_scales)
         load_weight(0, wo_words, wo_scales)
-        for c in range(3, CHUNKS):
-            load_x(c)
+        for u in range(3, len(units)):
+            load_x(u)
 
-        nc.vector.tensor_copy(out=bias_rows_f32[:], in_=bias_rows[:])
-        bias_t = psum.tile([P, P], F32, tag="x_t")
-        nc.tensor.transpose(bias_t[:], bias_rows_f32[:], identity[:])
-        nc.vector.tensor_copy(out=bias_cols[:], in_=bias_t[:, 0 : GATES * HALVES])
+        def bias_columns():
+            cols_ps = psum.tile([P, GATES * HALVES], F32, tag="out_t")
+            for block in range(GATES * HALVES):
+                nc.tensor.matmul(
+                    out=cols_ps[:, block : block + 1],
+                    lhsT=bias_row[:, block * P : (block + 1) * P],
+                    rhs=ones[:, 0:1],
+                    start=True,
+                    stop=True,
+                )
+            nc.vector.tensor_copy(out=bias_cols[:], in_=cols_ps[:])
 
+        def bias_everywhere():
+            wide_ps = psum.tile([P, GATES * FEATURES], F32, tag="out_t")
+            nc.tensor.matmul(out=wide_ps[:], lhsT=ones[:], rhs=bias_row[:], start=True, stop=True)
+            nc.vector.tensor_copy(out=bias_wide[:], in_=wide_ps[:])
+
+        grouped_of = {}
         product_of = {}
-        for step in range(CHUNKS + STORE_LAG):
-            if step < CHUNKS:
-                grouped = transpose_x(step)
-            if step >= STORE_LAG:
-                out_t = transpose_back(step - STORE_LAG, product_of[step - STORE_LAG])
-                store(step - STORE_LAG, out_t)
-            if step < CHUNKS:
-                quantise_x(step, grouped)
-            if GATE_LAG <= step < CHUNKS + GATE_LAG:
-                product_of[step - GATE_LAG] = cell(step - GATE_LAG)
+        pre_of = {}
+
+        def way_in(u):
+            if u < len(units):
+                grouped_of[u] = transpose_x(u)
+
+        def quantise(u):
+            if u < len(units):
+                quantise_x(u, grouped_of[u])
+
+        way_in(0)
+        quantise(0)
+        way_in(1)
+        quantise(1)
+        bias_columns()
+        way_in(2)
+        for j in range(n_w):
+            product_of[j] = cell_w(j, multiply_w(j))
+            quantise(j + 2)
+            way_in(j + 3)
+            if j == 1:
+                bias_everywhere()
+            if j == n_w - 1:
+                pre_of[n_w] = prepare_x(n_w)
+            if j >= BACK_LAG:
+                back(j - BACK_LAG, product_of[j - BACK_LAG])
+        for j in range(n_w + 1, len(chunks)):
+            pre_of[j] = prepare_x(j)
+        back(n_w - 2, product_of[n_w - 2])
+        cell_x(n_w, pre_of[n_w])
+        back(n_w - 1, product_of[n_w - 1])
+        for j in range(n_w + 1, len(chunks)):
+            cell_x(j, pre_of[j])

@@ -36,6 +36,8 @@ X_UNITS = [1, 1, 2, 2, 2, 2, 2, 2, 2]
 assert sum(X_UNITS) == ROW_TILES
 BACK_LAG = 2
 PRODUCTS = 4
+WARM_UPS = 16
+HEAD_UNITS = 3
 
 FLOPS = 2 * ROWS * K * GATES * FEATURES
 BYTES = ROWS * K * 2 + GATES * (K * FEATURES // 2 + K // 32 * FEATURES + FEATURES * 2) + ROWS * FEATURES * 4
@@ -83,9 +85,9 @@ def tile_mdlstm_kernel(
         identity = keep.tile([P, P], F32)
         table_warmer = keep.tile([P, 2], F32)
 
-        def load_x(u):
+        def load_x(u, queue):
             first, size = units[u]
-            nc.sync.dma_start(out=x_sb[:, first : first + size, :], in_=x_rows[:, first : first + size, :])
+            queue.dma_start(out=x_sb[:, first : first + size, :], in_=x_rows[:, first : first + size, :])
 
         def load_weight(gate, words, scales):
             nc.sync.dma_start(
@@ -229,21 +231,23 @@ def tile_mdlstm_kernel(
             )
             nc.sync.dma_start(out=out_rows[:, first : first + tiles, :], in_=out_sb[:, first : first + tiles, :])
 
+        nc.gpsimd.memset(ones[:], 1.0)
         nc.vector.memset(table_warmer[:], 0.0)
         nc.vector.memset(w_scales[:].bitcast(I32), 0)
         nc.vector.memset(bias_row[:], 0.0)
-        nc.vector.memset(ones[:], 1.0)
         make_identity(nc, identity[:])
+        warm_ps = acc_pool.tile([P, BANK], F32, tag="acc")
+        for i in range(WARM_UPS):
+            nc.tensor.matmul(out=warm_ps[:, 0:P], lhsT=ones[:], rhs=ones[:], start=True, stop=True)
+        for u in range(HEAD_UNITS):
+            load_x(u, nc.scalar)
         nc.scalar.dma_start(out=bias_row[0:1, 0:FEATURES], in_=biaso.rearrange("(a n) -> a n", a=1))
         nc.scalar.dma_start(out=bias_row[0:1, FEATURES:], in_=biasc.rearrange("(a n) -> a n", a=1))
         nc.scalar.activation(out=table_warmer[:, 1:2], in_=table_warmer[:, 0:1], func=SIGMOID)
-        load_x(0)
-        load_x(1)
-        load_x(2)
         load_weight(1, wc_words, wc_scales)
         load_weight(0, wo_words, wo_scales)
-        for u in range(3, len(units)):
-            load_x(u)
+        for u in range(HEAD_UNITS, len(units)):
+            load_x(u, nc.sync)
 
         def bias_columns():
             cols_ps = psum.tile([P, GATES * HALVES], F32, tag="out_t")

@@ -225,11 +225,21 @@ def tile_mdlstm_kernel(
             x_tanh = gates.tile([P, UNIT, FEATURES], F32)
             nc.scalar.activation(out=sig[:, :tiles, FEATURES:], in_=pre[:, :tiles, FEATURES:], func=SIGMOID)
             nc.scalar.activation(out=sig[:, :tiles, :FEATURES], in_=pre[:, :tiles, :FEATURES], func=SIGMOID)
-            nc.scalar.activation(out=x_tanh[:, :tiles, :], in_=sig[:, :tiles, FEATURES:], func=TANH)
-            nc.vector.tensor_tensor(
-                out=out_sb[:, first : first + tiles, :], in0=sig[:, :tiles, :FEATURES], in1=x_tanh[:, :tiles, :], op=MULT
-            )
-            nc.sync.dma_start(out=out_rows[:, first : first + tiles, :], in_=out_sb[:, first : first + tiles, :])
+            pieces = 2 if j == len(chunks) - 1 else 1
+            width = FEATURES // pieces
+            for piece in range(pieces):
+                cols = slice(piece * width, (piece + 1) * width)
+                nc.scalar.activation(
+                    out=x_tanh[:, :tiles, cols],
+                    in_=sig[:, :tiles, FEATURES + piece * width : FEATURES + (piece + 1) * width],
+                    func=TANH,
+                )
+                nc.vector.tensor_tensor(
+                    out=out_sb[:, first : first + tiles, cols], in0=sig[:, :tiles, cols], in1=x_tanh[:, :tiles, cols], op=MULT
+                )
+                nc.sync.dma_start(
+                    out=out_rows[:, first : first + tiles, cols], in_=out_sb[:, first : first + tiles, cols]
+                )
 
         nc.gpsimd.memset(ones[:], 1.0)
         nc.vector.memset(table_warmer[:], 0.0)
@@ -288,7 +298,7 @@ def tile_mdlstm_kernel(
             product_of[j] = cell_w(j, multiply_w(j))
             quantise(j + 2)
             way_in(j + 3)
-            if j == 1:
+            if j == 2:
                 bias_everywhere()
             if j == n_w - 1:
                 pre_of[n_w] = prepare_x(n_w)

@@ -27,12 +27,12 @@ QUADRANTS = 4
 UNIT = 2
 BANK = 512
 
-W_CHUNKS = [1, 1, 2, 2, 2, 2, 2]
+W_CHUNKS = [2, 2, 2, 2, 2, 2]
 X_GROUPS = [2, 1, 1]
 assert sum(W_CHUNKS) + sum(X_GROUPS) == ROW_TILES
 MAX_ROWS = max(W_CHUNKS) * P
 SCALAR_COPIES = 2
-X_UNITS = [1, 1, 2, 2, 2, 2, 2, 2, 2]
+X_UNITS = [2, 2, 2, 2, 2, 2, 2, 2]
 assert sum(X_UNITS) == ROW_TILES
 BACK_LAG = 2
 PRODUCTS = 4

@@ -31,7 +31,7 @@ W_CHUNKS = [2, 2, 2, 2, 2, 2]
 X_GROUPS = [2, 1, 1]
 assert sum(W_CHUNKS) + sum(X_GROUPS) == ROW_TILES
 MAX_ROWS = max(W_CHUNKS) * P
-SCALAR_COPIES = 2
+SCALAR_COPIES = 3
 X_UNITS = [2, 2, 2, 2, 2, 2, 2, 2]
 assert sum(X_UNITS) == ROW_TILES
 BACK_LAG = 2

@@ -296,8 +296,12 @@ def tile_mdlstm_kernel(
         way_in(2)
         for j in range(n_w):
             product_of[j] = cell_w(j, multiply_w(j))
-            quantise(j + 2)
-            way_in(j + 3)
+            if j < BACK_LAG:
+                quantise(j + 2)
+                way_in(j + 3)
+            else:
+                way_in(j + 3)
+                quantise(j + 2)
             if j == 2:
                 bias_everywhere()
             if j == n_w - 1:

@@ -31,12 +31,12 @@ W_CHUNKS = [2, 2, 2, 2, 2, 2]
 X_GROUPS = [2, 1, 1]
 assert sum(W_CHUNKS) + sum(X_GROUPS) == ROW_TILES
 MAX_ROWS = max(W_CHUNKS) * P
-SCALAR_COPIES = 3
+SCALAR_COPIES = 2
 X_UNITS = [2, 2, 2, 2, 2, 2, 2, 2]
 assert sum(X_UNITS) == ROW_TILES
 BACK_LAG = 2
 PRODUCTS = 4
-WARM_UPS = 16
+WARM_UPS = 10
 HEAD_UNITS = 3
 
 FLOPS = 2 * ROWS * K * GATES * FEATURES
@@ -118,6 +118,27 @@ def tile_mdlstm_kernel(
             else:
                 nc.vector.tensor_copy(out=target, in_=source)
             return grouped
+
+        def first_pair():
+            grouped = stage.tile([P, UNIT * P * 4], BF16, align_bytes=64)
+            for i in range(UNIT):
+                words = x_sb[:, i, :].bitcast(F32)
+                x_t = psum.tile([P, 2, P], F32, tag="x_t")
+                for parity in range(2):
+                    nc.tensor.transpose(x_t[:, parity, :], words[:, parity:WORDS:2], identity[:])
+                target = grouped[:, i * P * 4 : (i + 1) * P * 4].bitcast(F32).rearrange("p (r w) -> p r w", w=2)
+                source = x_t[:].rearrange("p w r -> p r w")
+                if i == 0:
+                    nc.scalar.copy(out=target, in_=source)
+                else:
+                    nc.vector.tensor_copy(out=target, in_=source)
+            for i in range(UNIT):
+                rows = slice(i * P, (i + 1) * P)
+                nc.vector.quantize_mx(
+                    out=x_codes[:, rows].bitcast(FP8X4),
+                    scales=x_scales[:, rows],
+                    in_=grouped[:, i * P * 4 : (i + 1) * P * 4],
+                )
 
         def quantise_x(u, grouped):
             first, tiles = units[u]
@@ -244,32 +265,34 @@ def tile_mdlstm_kernel(
         nc.gpsimd.memset(ones[:], 1.0)
         nc.vector.memset(table_warmer[:], 0.0)
         nc.vector.memset(w_scales[:].bitcast(I32), 0)
-        nc.vector.memset(bias_row[:], 0.0)
+        nc.vector.memset(bias_row[:].bitcast(I32), 0)
         make_identity(nc, identity[:])
         warm_ps = acc_pool.tile([P, BANK], F32, tag="acc")
         for i in range(WARM_UPS):
             nc.tensor.matmul(out=warm_ps[:, 0:P], lhsT=ones[:], rhs=ones[:], start=True, stop=True)
-        for u in range(HEAD_UNITS):
-            load_x(u, nc.scalar)
-        nc.scalar.dma_start(out=bias_row[0:1, 0:FEATURES], in_=biaso.rearrange("(a n) -> a n", a=1))
-        nc.scalar.dma_start(out=bias_row[0:1, FEATURES:], in_=biasc.rearrange("(a n) -> a n", a=1))
+        nc.gpsimd.dma_start(out=bias_row[0:1, FEATURES:], in_=biasc.rearrange("(a n) -> a n", a=1))
+        nc.gpsimd.dma_start(out=bias_row[0:1, 0:FEATURES], in_=biaso.rearrange("(a n) -> a n", a=1))
         nc.scalar.activation(out=table_warmer[:, 1:2], in_=table_warmer[:, 0:1], func=SIGMOID)
+        load_x(0, nc.sync)
         load_weight(1, wc_words, wc_scales)
+        for u in range(1, HEAD_UNITS):
+            load_x(u, nc.sync)
         load_weight(0, wo_words, wo_scales)
         for u in range(HEAD_UNITS, len(units)):
             load_x(u, nc.sync)
 
-        def bias_columns():
-            cols_ps = psum.tile([P, GATES * HALVES], F32, tag="out_t")
-            for block in range(GATES * HALVES):
+        def bias_columns(gate):
+            cols_ps = psum.tile([P, HALVES], F32, tag="out_t")
+            for half in range(HALVES):
+                block = gate * HALVES + half
                 nc.tensor.matmul(
-                    out=cols_ps[:, block : block + 1],
+                    out=cols_ps[:, half : half + 1],
                     lhsT=bias_row[:, block * P : (block + 1) * P],
                     rhs=ones[:, 0:1],
                     start=True,
                     stop=True,
                 )
-            nc.vector.tensor_copy(out=bias_cols[:], in_=cols_ps[:])
+            nc.vector.tensor_copy(out=bias_cols[:, gate * HALVES : (gate + 1) * HALVES], in_=cols_ps[:])
 
         def bias_everywhere():
             wide_ps = psum.tile([P, GATES * FEATURES], F32, tag="out_t")
@@ -288,14 +311,16 @@ def tile_mdlstm_kernel(
             if u < len(units):
                 quantise_x(u, grouped_of[u])
 
-        way_in(0)
-        quantise(0)
+        first_pair()
         way_in(1)
+        bias_columns(1)
         quantise(1)
-        bias_columns()
         way_in(2)
         for j in range(n_w):
-            product_of[j] = cell_w(j, multiply_w(j))
+            acc = multiply_w(j)
+            if j == 0:
+                bias_columns(0)
+            product_of[j] = cell_w(j, acc)
             if j < BACK_LAG:
                 quantise(j + 2)
                 way_in(j + 3)

@@ -36,8 +36,7 @@ X_UNITS = [2, 2, 2, 2, 2, 2, 2, 2]
 assert sum(X_UNITS) == ROW_TILES
 BACK_LAG = 2
 PRODUCTS = 4
-WARM_UPS = 10
-HEAD_UNITS = 3
+WARM_UPS = 12
 
 FLOPS = 2 * ROWS * K * GATES * FEATURES
 BYTES = ROWS * K * 2 + GATES * (K * FEATURES // 2 + K // 32 * FEATURES + FEATURES * 2) + ROWS * FEATURES * 4
@@ -81,7 +80,7 @@ def tile_mdlstm_kernel(
         bias_row = keep.tile([P, GATES * FEATURES], BF16)
         ones = keep.tile([P, P], BF16)
         bias_cols = keep.tile([P, GATES * HALVES], F32)
-        bias_wide = keep.tile([P, GATES * FEATURES], F32)
+        bias_wide = keep.tile([P, GATES * FEATURES], BF16)
         identity = keep.tile([P, P], F32)
         table_warmer = keep.tile([P, 2], F32)
 
@@ -110,6 +109,10 @@ def tile_mdlstm_kernel(
                 words = x_sb[:, first + i, :].bitcast(F32)
                 for parity in range(2):
                     nc.tensor.transpose(x_t[:, i, parity, :], words[:, parity:WORDS:2], identity[:])
+            return x_t
+
+        def copy_x(u, x_t):
+            first, tiles = units[u]
             grouped = stage.tile([P, UNIT * P * 4], BF16, align_bytes=64)
             target = grouped[:, : tiles * P * 4].bitcast(F32).rearrange("p (i r w) -> p i r w", i=tiles, w=2)
             source = x_t[:, :tiles].rearrange("p i w r -> p i r w")
@@ -123,7 +126,7 @@ def tile_mdlstm_kernel(
             grouped = stage.tile([P, UNIT * P * 4], BF16, align_bytes=64)
             for i in range(UNIT):
                 words = x_sb[:, i, :].bitcast(F32)
-                x_t = psum.tile([P, 2, P], F32, tag="x_t")
+                x_t = psum.tile([P, 2, P], F32, tag="out_t")
                 for parity in range(2):
                     nc.tensor.transpose(x_t[:, parity, :], words[:, parity:WORDS:2], identity[:])
                 target = grouped[:, i * P * 4 : (i + 1) * P * 4].bitcast(F32).rearrange("p (r w) -> p r w", w=2)
@@ -149,12 +152,12 @@ def tile_mdlstm_kernel(
                 in_=grouped[:, : tiles * P * 4],
             )
 
-        def multiply_w(j):
+        def multiply_w(j, only=(1, 0)):
             kind, first, tiles = chunks[j]
             rows = tiles * P
             cols = slice(first * P, first * P + rows)
             views = {}
-            for gate in (1, 0):
+            for gate in only:
                 halves = []
                 if tiles <= UNIT:
                     bank = acc_pool.tile([P, HALVES, UNIT * P], F32, tag="acc")
@@ -270,15 +273,15 @@ def tile_mdlstm_kernel(
         warm_ps = acc_pool.tile([P, BANK], F32, tag="acc")
         for i in range(WARM_UPS):
             nc.tensor.matmul(out=warm_ps[:, 0:P], lhsT=ones[:], rhs=ones[:], start=True, stop=True)
-        nc.gpsimd.dma_start(out=bias_row[0:1, FEATURES:], in_=biasc.rearrange("(a n) -> a n", a=1))
-        nc.gpsimd.dma_start(out=bias_row[0:1, 0:FEATURES], in_=biaso.rearrange("(a n) -> a n", a=1))
         nc.scalar.activation(out=table_warmer[:, 1:2], in_=table_warmer[:, 0:1], func=SIGMOID)
         load_x(0, nc.sync)
+        load_x(1, nc.sync)
         load_weight(1, wc_words, wc_scales)
-        for u in range(1, HEAD_UNITS):
-            load_x(u, nc.sync)
+        load_x(2, nc.sync)
+        nc.sync.dma_start(out=bias_row[0:1, FEATURES:], in_=biasc.rearrange("(a n) -> a n", a=1))
         load_weight(0, wo_words, wo_scales)
-        for u in range(HEAD_UNITS, len(units)):
+        nc.sync.dma_start(out=bias_row[0:1, 0:FEATURES], in_=biaso.rearrange("(a n) -> a n", a=1))
+        for u in range(3, len(units)):
             load_x(u, nc.sync)
 
         def bias_columns(gate):
@@ -295,7 +298,7 @@ def tile_mdlstm_kernel(
             nc.vector.tensor_copy(out=bias_cols[:, gate * HALVES : (gate + 1) * HALVES], in_=cols_ps[:])
 
         def bias_everywhere():
-            wide_ps = psum.tile([P, GATES * FEATURES], F32, tag="out_t")
+            wide_ps = psum.tile([P, GATES * FEATURES], BF16, tag="out_t")
             nc.tensor.matmul(out=wide_ps[:], lhsT=ones[:], rhs=bias_row[:], start=True, stop=True)
             nc.vector.tensor_copy(out=bias_wide[:], in_=wide_ps[:])
 
@@ -305,7 +308,7 @@ def tile_mdlstm_kernel(
 
         def way_in(u):
             if u < len(units):
-                grouped_of[u] = transpose_x(u)
+                grouped_of[u] = copy_x(u, transpose_x(u))
 
         def quantise(u):
             if u < len(units):
@@ -313,15 +316,18 @@ def tile_mdlstm_kernel(
 
         first_pair()
         way_in(1)
+        third = transpose_x(2)
         bias_columns(1)
+        acc = multiply_w(0, (1,))
         quantise(1)
-        way_in(2)
+        grouped_of[2] = copy_x(2, third)
+        acc.update(multiply_w(0, (0,)))
+        bias_columns(0)
         for j in range(n_w):
-            acc = multiply_w(j)
-            if j == 0:
-                bias_columns(0)
+            if j > 0:
+                acc = multiply_w(j)
             product_of[j] = cell_w(j, acc)
-            if j < BACK_LAG:
+            if j == 0:
                 quantise(j + 2)
                 way_in(j + 3)
             else:

@@ -21,21 +21,16 @@ K = 512
 FEATURES = 256
 ROW_TILES = ROWS // P
 HALVES = FEATURES // P
+O, C = 0, 1
 GATES = 2
 WORDS = K // 2
 QUADRANTS = 4
-UNIT = 2
+PAIR = 2
+PAIR_ROWS = PAIR * P
+PAIRS = ROW_TILES // PAIR
 BANK = 512
 
-W_CHUNKS = [2, 2, 2, 2, 2, 2]
-X_GROUPS = [2, 1, 1]
-assert sum(W_CHUNKS) + sum(X_GROUPS) == ROW_TILES
-MAX_ROWS = max(W_CHUNKS) * P
-SCALAR_COPIES = 2
-X_UNITS = [2, 2, 2, 2, 2, 2, 2, 2]
-assert sum(X_UNITS) == ROW_TILES
-BACK_LAG = 2
-PRODUCTS = 4
+WAYS = "WMWMWMMX"
 WARM_UPS = 12
 
 FLOPS = 2 * ROWS * K * GATES * FEATURES
@@ -49,24 +44,10 @@ def tile_mdlstm_kernel(
     x_rows = x.flatten_outer_dims().rearrange("(p t) k -> p t k", t=ROW_TILES)
     out_rows = out.flatten_outer_dims().rearrange("(p t) n -> p t n", t=ROW_TILES)
 
-    chunks = []
-    first_tile = 0
-    for kind, sizes in (("W", W_CHUNKS), ("X", X_GROUPS)):
-        for size in sizes:
-            chunks.append((kind, first_tile, size))
-            first_tile += size
-    units = []
-    first_tile = 0
-    for size in X_UNITS:
-        units.append((first_tile, size))
-        first_tile += size
-    n_w = len(W_CHUNKS)
-
     with ExitStack() as ctx:
         keep = ctx.enter_context(tc.tile_pool(name="keep", bufs=1))
-        stage = ctx.enter_context(tc.tile_pool(name="stage", bufs=3))
-        gates = ctx.enter_context(tc.tile_pool(name="gates", bufs=3))
-        products = ctx.enter_context(tc.tile_pool(name="products", bufs=PRODUCTS))
+        stage = ctx.enter_context(tc.tile_pool(name="stage", bufs=4))
+        gates = ctx.enter_context(tc.tile_pool(name="gates", bufs=4))
         psum = ctx.enter_context(tc.psum_pool(name="psum", bufs=2))
         acc_pool = ctx.enter_context(tc.psum_pool(name="acc_pool", bufs=4))
         ctx.enter_context(tc.manual_schedule())
@@ -84,9 +65,11 @@ def tile_mdlstm_kernel(
         identity = keep.tile([P, P], F32)
         table_warmer = keep.tile([P, 2], F32)
 
-        def load_x(u, queue):
-            first, size = units[u]
-            queue.dma_start(out=x_sb[:, first : first + size, :], in_=x_rows[:, first : first + size, :])
+        def tiles_of(j):
+            return slice(j * PAIR, (j + 1) * PAIR)
+
+        def load_x(j):
+            nc.sync.dma_start(out=x_sb[:, tiles_of(j), :], in_=x_rows[:, tiles_of(j), :])
 
         def load_weight(gate, words, scales):
             nc.sync.dma_start(
@@ -102,168 +85,190 @@ def tile_mdlstm_kernel(
                     in_=scale_rows[4 * quadrant : 4 * quadrant + 4, :].bitcast(I32),
                 )
 
-        def transpose_x(u):
-            first, tiles = units[u]
-            x_t = psum.tile([P, UNIT, 2, P], F32, tag="x_t")
-            for i in range(tiles):
-                words = x_sb[:, first + i, :].bitcast(F32)
-                for parity in range(2):
-                    nc.tensor.transpose(x_t[:, i, parity, :], words[:, parity:WORDS:2], identity[:])
-            return x_t
-
-        def copy_x(u, x_t):
-            first, tiles = units[u]
-            grouped = stage.tile([P, UNIT * P * 4], BF16, align_bytes=64)
-            target = grouped[:, : tiles * P * 4].bitcast(F32).rearrange("p (i r w) -> p i r w", i=tiles, w=2)
-            source = x_t[:, :tiles].rearrange("p i w r -> p i r w")
-            if u < SCALAR_COPIES:
-                nc.scalar.copy(out=target, in_=source)
-            else:
-                nc.vector.tensor_copy(out=target, in_=source)
-            return grouped
-
-        def first_pair():
-            grouped = stage.tile([P, UNIT * P * 4], BF16, align_bytes=64)
-            for i in range(UNIT):
-                words = x_sb[:, i, :].bitcast(F32)
-                x_t = psum.tile([P, 2, P], F32, tag="out_t")
-                for parity in range(2):
-                    nc.tensor.transpose(x_t[:, parity, :], words[:, parity:WORDS:2], identity[:])
-                target = grouped[:, i * P * 4 : (i + 1) * P * 4].bitcast(F32).rearrange("p (r w) -> p r w", w=2)
-                source = x_t[:].rearrange("p w r -> p r w")
-                if i == 0:
-                    nc.scalar.copy(out=target, in_=source)
-                else:
-                    nc.vector.tensor_copy(out=target, in_=source)
-            for i in range(UNIT):
-                rows = slice(i * P, (i + 1) * P)
-                nc.vector.quantize_mx(
-                    out=x_codes[:, rows].bitcast(FP8X4),
-                    scales=x_scales[:, rows],
-                    in_=grouped[:, i * P * 4 : (i + 1) * P * 4],
-                )
-
-        def quantise_x(u, grouped):
-            first, tiles = units[u]
-            rows = slice(first * P, (first + tiles) * P)
-            nc.vector.quantize_mx(
-                out=x_codes[:, rows].bitcast(FP8X4),
-                scales=x_scales[:, rows],
-                in_=grouped[:, : tiles * P * 4],
+        def load_bias(gate, bias):
+            nc.sync.dma_start(
+                out=bias_row[0:1, gate * FEATURES : (gate + 1) * FEATURES], in_=bias.rearrange("(a n) -> a n", a=1)
             )
 
-        def multiply_w(j, only=(1, 0)):
-            kind, first, tiles = chunks[j]
-            rows = tiles * P
-            cols = slice(first * P, first * P + rows)
-            views = {}
-            for gate in only:
-                halves = []
-                if tiles <= UNIT:
-                    bank = acc_pool.tile([P, HALVES, UNIT * P], F32, tag="acc")
-                    for half in range(HALVES):
-                        halves.append(bank[:, half, :rows])
-                else:
-                    for half in range(HALVES):
-                        bank = acc_pool.tile([P, BANK], F32, tag="acc")
-                        halves.append(bank[:, :rows])
-                for half in range(HALVES):
-                    block = gate * HALVES + half
-                    nc.tensor.matmul_mx(
-                        out=halves[half],
-                        lhsT=w_words[:, block * P * 2 : (block + 1) * P * 2].bitcast(FP4X4),
-                        lhsT_scale=w_scales[:, block * P : (block + 1) * P],
-                        rhs=x_codes[:, cols].bitcast(FP8X4),
-                        rhs_scale=x_scales[:, cols],
-                        start=True,
-                        stop=True,
-                    )
-                views[gate] = halves
-            return views
+        turned = {}
+        grouped = {}
 
-        def cell_w(j, acc):
-            kind, first, tiles = chunks[j]
-            rows = tiles * P
-            o_sig = gates.tile([P, HALVES, MAX_ROWS], F32)
-            c_sig = gates.tile([P, HALVES, MAX_ROWS], F32)
-            c_tanh = gates.tile([P, HALVES, MAX_ROWS], F32)
-            product = products.tile([P, HALVES, MAX_ROWS], F32)
+        def turn_tile(t, target):
+            words = x_sb[:, t, :].bitcast(F32)
+            for parity in range(2):
+                nc.tensor.transpose(target[:, parity, :], words[:, parity:WORDS:2], identity[:])
 
-            def sigmoid(gate, half, result):
+        def turn(j):
+            if j < PAIRS:
+                x_t = psum.tile([P, PAIR, 2, P], F32, tag="x_t")
+                for i in range(PAIR):
+                    turn_tile(j * PAIR + i, x_t[:, i])
+                turned[j] = x_t
+
+        def group(j, copy):
+            if j < PAIRS:
+                words = stage.tile([P, PAIR_ROWS * 4], BF16, align_bytes=64)
+                grouped[j] = words
+                copy(
+                    out=words[:].bitcast(F32).rearrange("p (i r w) -> p i r w", i=PAIR, w=2),
+                    in_=turned[j][:].rearrange("p i w r -> p i r w"),
+                )
+
+        def quantise_rows(first_row, rows, source):
+            nc.vector.quantize_mx(
+                out=x_codes[:, first_row : first_row + rows].bitcast(FP8X4),
+                scales=x_scales[:, first_row : first_row + rows],
+                in_=source,
+            )
+
+        def quantise(j):
+            if j < PAIRS:
+                quantise_rows(j * PAIR_ROWS, PAIR_ROWS, grouped[j][:])
+
+        def first_pair():
+            both = stage.tile([P, PAIR_ROWS * 4], BF16, align_bytes=64)
+            for i, copy in enumerate((nc.scalar.copy, nc.vector.tensor_copy)):
+                x_t = psum.tile([P, 2, P], F32, tag="out_t")
+                turn_tile(i, x_t)
+                copy(
+                    out=both[:, i * P * 4 : (i + 1) * P * 4].bitcast(F32).rearrange("p (r w) -> p r w", w=2),
+                    in_=x_t[:].rearrange("p w r -> p r w"),
+                )
+            for i in range(PAIR):
+                quantise_rows(i * P, P, both[:, i * P * 4 : (i + 1) * P * 4])
+
+        sums = {}
+
+        def multiply_by_feature(j, gate):
+            cols = slice(j * PAIR_ROWS, (j + 1) * PAIR_ROWS)
+            bank = acc_pool.tile([P, HALVES, PAIR_ROWS], F32, tag="acc")
+            for half in range(HALVES):
                 block = gate * HALVES + half
-                nc.scalar.activation(
-                    out=result[:, half, :rows],
-                    in_=acc[gate][half],
-                    func=SIGMOID,
-                    bias=bias_cols[:, block : block + 1],
-                )
-
-            def multiply(half):
-                nc.gpsimd.tensor_tensor(
-                    out=product[:, half, :rows], in0=o_sig[:, half, :rows], in1=c_tanh[:, half, :rows], op=MULT
-                )
-
-            sigmoid(1, 0, c_sig)
-            sigmoid(1, 1, c_sig)
-            sigmoid(0, 0, o_sig)
-            nc.scalar.activation(out=c_tanh[:, :, :rows], in_=c_sig[:, :, :rows], func=TANH)
-            multiply(0)
-            sigmoid(0, 1, o_sig)
-            multiply(1)
-            return product
-
-        def back(j, product):
-            kind, first, tiles = chunks[j]
-            chunk_first = first
-            out_t = psum.tile([P, UNIT, FEATURES], F32, tag="out_t")
-            for i in range(tiles):
-                r0 = (first + i - chunk_first) * P
-                for half in range(HALVES):
-                    nc.tensor.transpose(
-                        out_t[:, i, half * P : (half + 1) * P], product[:, half, r0 : r0 + P], identity[:]
-                    )
-            nc.vector.tensor_copy(out=out_sb[:, first : first + tiles, :], in_=out_t[:, :tiles, :])
-            nc.sync.dma_start(out=out_rows[:, first : first + tiles, :], in_=out_sb[:, first : first + tiles, :])
-
-        def prepare_x(j):
-            kind, first, tiles = chunks[j]
-            pre = gates.tile([P, UNIT, GATES * FEATURES], F32)
-            for i in range(tiles):
-                rows = slice((first + i) * P, (first + i + 1) * P)
-                acc = psum.tile([P, GATES * FEATURES], F32, tag="x_t")
                 nc.tensor.matmul_mx(
-                    out=acc[:],
-                    lhsT=x_codes[:, rows].bitcast(FP8X4),
-                    lhsT_scale=x_scales[:, rows],
-                    rhs=w_words[:].bitcast(FP4X4),
-                    rhs_scale=w_scales[:],
+                    out=bank[:, half, :],
+                    lhsT=w_words[:, block * P * 2 : (block + 1) * P * 2].bitcast(FP4X4),
+                    lhsT_scale=w_scales[:, block * P : (block + 1) * P],
+                    rhs=x_codes[:, cols].bitcast(FP8X4),
+                    rhs_scale=x_scales[:, cols],
                     start=True,
                     stop=True,
                 )
-                nc.vector.tensor_tensor(out=pre[:, i, :], in0=acc[:], in1=bias_wide[:], op=ADD)
-            return pre
+            sums[j, gate] = bank
 
-        def cell_x(j, pre):
-            kind, first, tiles = chunks[j]
-            sig = gates.tile([P, UNIT, GATES * FEATURES], F32)
-            x_tanh = gates.tile([P, UNIT, FEATURES], F32)
-            nc.scalar.activation(out=sig[:, :tiles, FEATURES:], in_=pre[:, :tiles, FEATURES:], func=SIGMOID)
-            nc.scalar.activation(out=sig[:, :tiles, :FEATURES], in_=pre[:, :tiles, :FEATURES], func=SIGMOID)
-            pieces = 2 if j == len(chunks) - 1 else 1
-            width = FEATURES // pieces
-            for piece in range(pieces):
-                cols = slice(piece * width, (piece + 1) * width)
-                nc.scalar.activation(
-                    out=x_tanh[:, :tiles, cols],
-                    in_=sig[:, :tiles, FEATURES + piece * width : FEATURES + (piece + 1) * width],
-                    func=TANH,
-                )
+        def multiply_by_row(t, target, first_col, cols):
+            rows = slice(t * P, (t + 1) * P)
+            nc.tensor.matmul_mx(
+                out=target,
+                lhsT=x_codes[:, rows].bitcast(FP8X4),
+                lhsT_scale=x_scales[:, rows],
+                rhs=w_words[:, first_col * 2 : (first_col + cols) * 2].bitcast(FP4X4),
+                rhs_scale=w_scales[:, first_col : first_col + cols],
+                start=True,
+                stop=True,
+            )
+
+        def multiply(j):
+            if WAYS[j] == "X":
+                for i in range(PAIR):
+                    bank = acc_pool.tile([P, GATES * FEATURES], F32, tag="acc")
+                    multiply_by_row(j * PAIR + i, bank[:], 0, GATES * FEATURES)
+                    sums[j, i] = bank
+                return
+            multiply_by_feature(j, C)
+            if WAYS[j] == "W":
+                multiply_by_feature(j, O)
+            else:
+                bank = acc_pool.tile([P, PAIR, FEATURES], F32, tag="acc")
+                for i in range(PAIR):
+                    multiply_by_row(j * PAIR + i, bank[:, i, :], O * FEATURES, FEATURES)
+                sums[j, O] = bank
+
+        biased = {}
+        sig_o = {}
+        to_turn = {}
+
+        def add_bias(j):
+            if WAYS[j] == "M":
+                biased_o = gates.tile([P, PAIR, FEATURES], F32)
+                biased[j] = biased_o
                 nc.vector.tensor_tensor(
-                    out=out_sb[:, first : first + tiles, cols], in0=sig[:, :tiles, cols], in1=x_tanh[:, :tiles, cols], op=MULT
+                    out=biased_o[:],
+                    in0=sums[j, O][:],
+                    in1=bias_wide[:, O * FEATURES : (O + 1) * FEATURES].unsqueeze(1).to_broadcast([P, PAIR, FEATURES]),
+                    op=ADD,
                 )
-                nc.sync.dma_start(
-                    out=out_rows[:, first : first + tiles, cols], in_=out_sb[:, first : first + tiles, cols]
+            if WAYS[j] == "X":
+                biased_both = gates.tile([P, PAIR, GATES * FEATURES], F32)
+                biased[j] = biased_both
+                for i in range(PAIR):
+                    nc.vector.tensor_tensor(out=biased_both[:, i, :], in0=sums[j, i][:], in1=bias_wide[:], op=ADD)
+
+        def sigmoid_by_feature(j, gate, half, result):
+            block = gate * HALVES + half
+            nc.scalar.activation(
+                out=result[:, half, :], in_=sums[j, gate][:, half, :], func=SIGMOID, bias=bias_cols[:, block : block + 1]
+            )
+
+        def cell(j):
+            c_sig = gates.tile([P, HALVES, PAIR_ROWS], F32)
+            c_tanh = gates.tile([P, HALVES, PAIR_ROWS], F32)
+            sigmoid_by_feature(j, C, 0, c_sig)
+            sigmoid_by_feature(j, C, 1, c_sig)
+            if WAYS[j] == "M":
+                nc.scalar.activation(out=c_tanh[:], in_=c_sig[:], func=TANH)
+                to_turn[j] = c_tanh
+                return
+            o_sig = gates.tile([P, HALVES, PAIR_ROWS], F32)
+            product = gates.tile([P, HALVES, PAIR_ROWS], F32)
+            sigmoid_by_feature(j, O, 0, o_sig)
+            nc.scalar.activation(out=c_tanh[:], in_=c_sig[:], func=TANH)
+            for half in range(HALVES):
+                if half == 1:
+                    sigmoid_by_feature(j, O, 1, o_sig)
+                nc.gpsimd.tensor_tensor(
+                    out=product[:, half, :], in0=o_sig[:, half, :], in1=c_tanh[:, half, :], op=MULT
                 )
+            to_turn[j] = product
+
+        def o_by_row(j):
+            o_rows = gates.tile([P, PAIR, FEATURES], F32)
+            sig_o[j] = o_rows
+            nc.scalar.activation(out=o_rows[:], in_=biased[j][:], func=SIGMOID)
+
+        def store(tiles, cols):
+            nc.sync.dma_start(out=out_rows[:, tiles, cols], in_=out_sb[:, tiles, cols])
+
+        def back(j):
+            if j < 0:
+                return
+            out_t = psum.tile([P, PAIR, FEATURES], F32, tag="out_t")
+            for i in range(PAIR):
+                for half in range(HALVES):
+                    nc.tensor.transpose(
+                        out_t[:, i, half * P : (half + 1) * P], to_turn[j][:, half, i * P : (i + 1) * P], identity[:]
+                    )
+            if WAYS[j] == "M":
+                nc.vector.tensor_tensor(out=out_sb[:, tiles_of(j), :], in0=out_t[:], in1=sig_o[j][:], op=MULT)
+            else:
+                nc.vector.tensor_copy(out=out_sb[:, tiles_of(j), :], in_=out_t[:])
+            store(tiles_of(j), slice(0, FEATURES))
+
+        def last_pair(j):
+            sig = gates.tile([P, PAIR, GATES * FEATURES], F32)
+            x_tanh = gates.tile([P, PAIR, FEATURES], F32)
+            for i in range(PAIR):
+                t = j * PAIR + i
+                nc.scalar.activation(out=sig[:, i, :], in_=biased[j][:, i, :], func=SIGMOID)
+                pieces = i + 1
+                width = FEATURES // pieces
+                for piece in range(pieces):
+                    cols = slice(piece * width, (piece + 1) * width)
+                    c_cols = slice(C * FEATURES + piece * width, C * FEATURES + (piece + 1) * width)
+                    nc.scalar.activation(out=x_tanh[:, i, cols], in_=sig[:, i, c_cols], func=TANH)
+                    nc.vector.tensor_tensor(
+                        out=out_sb[:, t, cols], in0=sig[:, i, cols], in1=x_tanh[:, i, cols], op=MULT
+                    )
+                    store(slice(t, t + 1), cols)
 
         nc.gpsimd.memset(ones[:], 1.0)
         nc.vector.memset(table_warmer[:], 0.0)
@@ -274,15 +279,15 @@ def tile_mdlstm_kernel(
         for i in range(WARM_UPS):
             nc.tensor.matmul(out=warm_ps[:, 0:P], lhsT=ones[:], rhs=ones[:], start=True, stop=True)
         nc.scalar.activation(out=table_warmer[:, 1:2], in_=table_warmer[:, 0:1], func=SIGMOID)
-        load_x(0, nc.sync)
-        load_x(1, nc.sync)
-        load_weight(1, wc_words, wc_scales)
-        load_x(2, nc.sync)
-        nc.sync.dma_start(out=bias_row[0:1, FEATURES:], in_=biasc.rearrange("(a n) -> a n", a=1))
-        load_weight(0, wo_words, wo_scales)
-        nc.sync.dma_start(out=bias_row[0:1, 0:FEATURES], in_=biaso.rearrange("(a n) -> a n", a=1))
-        for u in range(3, len(units)):
-            load_x(u, nc.sync)
+        load_x(0)
+        load_x(1)
+        load_weight(C, wc_words, wc_scales)
+        load_x(2)
+        load_bias(C, biasc)
+        load_weight(O, wo_words, wo_scales)
+        load_bias(O, biaso)
+        for j in range(3, PAIRS):
+            load_x(j)
 
         def bias_columns(gate):
             cols_ps = psum.tile([P, HALVES], F32, tag="out_t")
@@ -297,52 +302,41 @@ def tile_mdlstm_kernel(
                 )
             nc.vector.tensor_copy(out=bias_cols[:, gate * HALVES : (gate + 1) * HALVES], in_=cols_ps[:])
 
-        def bias_everywhere():
-            wide_ps = psum.tile([P, GATES * FEATURES], BF16, tag="out_t")
-            nc.tensor.matmul(out=wide_ps[:], lhsT=ones[:], rhs=bias_row[:], start=True, stop=True)
-            nc.vector.tensor_copy(out=bias_wide[:], in_=wide_ps[:])
-
-        grouped_of = {}
-        product_of = {}
-        pre_of = {}
-
-        def way_in(u):
-            if u < len(units):
-                grouped_of[u] = copy_x(u, transpose_x(u))
-
-        def quantise(u):
-            if u < len(units):
-                quantise_x(u, grouped_of[u])
-
         first_pair()
-        way_in(1)
-        third = transpose_x(2)
-        bias_columns(1)
-        acc = multiply_w(0, (1,))
+        turn(1)
+        group(1, nc.scalar.copy)
+        turn(2)
+        bias_columns(C)
+        multiply_by_feature(0, C)
         quantise(1)
-        grouped_of[2] = copy_x(2, third)
-        acc.update(multiply_w(0, (0,)))
-        bias_columns(0)
-        for j in range(n_w):
-            if j > 0:
-                acc = multiply_w(j)
-            product_of[j] = cell_w(j, acc)
-            if j == 0:
-                quantise(j + 2)
-                way_in(j + 3)
-            else:
-                way_in(j + 3)
-                quantise(j + 2)
-            if j == 2:
-                bias_everywhere()
-            if j == n_w - 1:
-                pre_of[n_w] = prepare_x(n_w)
-            if j >= BACK_LAG:
-                back(j - BACK_LAG, product_of[j - BACK_LAG])
-        for j in range(n_w + 1, len(chunks)):
-            pre_of[j] = prepare_x(j)
-        back(n_w - 2, product_of[n_w - 2])
-        cell_x(n_w, pre_of[n_w])
-        back(n_w - 1, product_of[n_w - 1])
-        for j in range(n_w + 1, len(chunks)):
-            cell_x(j, pre_of[j])
+        group(2, nc.vector.tensor_copy)
+        multiply_by_feature(0, O)
+        bias_columns(O)
+        cell(0)
+        quantise(2)
+        wide_ps = psum.tile([P, GATES * FEATURES], BF16, tag="out_t")
+        nc.tensor.matmul(out=wide_ps[:], lhsT=ones[:], rhs=bias_row[:], start=True, stop=True)
+        nc.vector.tensor_copy(out=bias_wide[:], in_=wide_ps[:])
+        turn(3)
+        for j in range(0, PAIRS - 2, 2):
+            multiply(j + 1)
+            group(j + 3, nc.vector.tensor_copy)
+            add_bias(j + 1)
+            cell(j + 1)
+            turn(j + 4)
+            group(j + 4, nc.vector.tensor_copy)
+            quantise(j + 3)
+            quantise(j + 4)
+            multiply(j + 2)
+            cell(j + 2)
+            o_by_row(j + 1)
+            turn(j + 5)
+            back(j - 1)
+            back(j)
+        multiply(PAIRS - 1)
+        add_bias(PAIRS - 2)
+        o_by_row(PAIRS - 2)
+        add_bias(PAIRS - 1)
+        back(PAIRS - 3)
+        back(PAIRS - 2)
+        last_pair(PAIRS - 1)

@@ -215,7 +215,8 @@ def tile_mdlstm_kernel(
             sigmoid_by_feature(j, C, 0, c_sig)
             sigmoid_by_feature(j, C, 1, c_sig)
             if WAYS[j] == "M":
-                nc.scalar.activation(out=c_tanh[:], in_=c_sig[:], func=TANH)
+                for half in range(HALVES):
+                    nc.scalar.activation(out=c_tanh[:, half, :], in_=c_sig[:, half, :], func=TANH)
                 to_turn[j] = c_tanh
                 return
             o_sig = gates.tile([P, HALVES, PAIR_ROWS], F32)
@@ -257,8 +258,9 @@ def tile_mdlstm_kernel(
             sig = gates.tile([P, PAIR, GATES * FEATURES], F32)
             x_tanh = gates.tile([P, PAIR, FEATURES], F32)
             for i in range(PAIR):
-                t = j * PAIR + i
                 nc.scalar.activation(out=sig[:, i, :], in_=biased[j][:, i, :], func=SIGMOID)
+            for i in range(PAIR):
+                t = j * PAIR + i
                 pieces = i + 1
                 width = FEATURES // pieces
                 for piece in range(pieces):

@@ -291,6 +291,7 @@ def tile_mdlstm_kernel(
         for j in range(3, PAIRS):
             load_x(j)
 
+
         def bias_columns(gate):
             cols_ps = psum.tile([P, HALVES], F32, tag="out_t")
             for half in range(HALVES):
@@ -316,27 +317,28 @@ def tile_mdlstm_kernel(
         bias_columns(O)
         cell(0)
         quantise(2)
+        multiply(1)
         wide_ps = psum.tile([P, GATES * FEATURES], BF16, tag="out_t")
         nc.tensor.matmul(out=wide_ps[:], lhsT=ones[:], rhs=bias_row[:], start=True, stop=True)
         nc.vector.tensor_copy(out=bias_wide[:], in_=wide_ps[:])
         turn(3)
+        turn(4)
         for j in range(0, PAIRS - 2, 2):
-            multiply(j + 1)
             group(j + 3, nc.vector.tensor_copy)
             add_bias(j + 1)
             cell(j + 1)
-            turn(j + 4)
             group(j + 4, nc.vector.tensor_copy)
             quantise(j + 3)
             quantise(j + 4)
             multiply(j + 2)
+            add_bias(j + 2)
             cell(j + 2)
             o_by_row(j + 1)
             turn(j + 5)
             back(j - 1)
             back(j)
-        multiply(PAIRS - 1)
-        add_bias(PAIRS - 2)
+            turn(j + 6)
+            multiply(j + 3)
         o_by_row(PAIRS - 2)
         add_bias(PAIRS - 1)
         back(PAIRS - 3)

from contextlib import ExitStack

import concourse.mybir as mybir
from concourse.masks import make_identity

F32 = mybir.dt.float32
BF16 = mybir.dt.bfloat16
I32 = mybir.dt.int32
U8 = mybir.dt.uint8
U32 = mybir.dt.uint32
FP8X4 = mybir.dt.float8_e4m3fn_x4
FP4X4 = mybir.dt.float4_e2m1fn_x4
SIGMOID = mybir.ActivationFunctionType.Sigmoid
TANH = mybir.ActivationFunctionType.Tanh
MULT = mybir.AluOpType.mult
ADD = mybir.AluOpType.add

P = 128
ROWS = 8 * 8 * 32
K = 512
FEATURES = 256
ROW_TILES = ROWS // P
HALVES = FEATURES // P
O, C = 0, 1
GATES = 2
WORDS = K // 2
QUADRANTS = 4
PAIR = 2
PAIR_ROWS = PAIR * P
PAIRS = ROW_TILES // PAIR
BANK = 512

WAYS = "WMWMWMMX"
WARM_UPS = 12

FLOPS = 2 * ROWS * K * GATES * FEATURES
BYTES = ROWS * K * 2 + GATES * (K * FEATURES // 2 + K // 32 * FEATURES + FEATURES * 2) + ROWS * FEATURES * 4


def tile_mdlstm_kernel(
    tc, x, wf, uf, biasf, wi, ui, biasi, wo_words, wo_scales, uo, biaso, wc_words, wc_scales, uc, biasc, out
):
    nc = tc.nc
    x_rows = x.flatten_outer_dims().rearrange("(p t) k -> p t k", t=ROW_TILES)
    out_rows = out.flatten_outer_dims().rearrange("(p t) n -> p t n", t=ROW_TILES)

    with ExitStack() as ctx:
        keep = ctx.enter_context(tc.tile_pool(name="keep", bufs=1))
        stage = ctx.enter_context(tc.tile_pool(name="stage", bufs=4))
        gates = ctx.enter_context(tc.tile_pool(name="gates", bufs=4))
        psum = ctx.enter_context(tc.psum_pool(name="psum", bufs=2))
        acc_pool = ctx.enter_context(tc.psum_pool(name="acc_pool", bufs=4))
        ctx.enter_context(tc.manual_schedule())

        x_sb = keep.tile([P, ROW_TILES, K], BF16)
        out_sb = keep.tile([P, ROW_TILES, FEATURES], F32)
        x_codes = keep.tile([P, ROWS], U32, align_bytes=64)
        x_scales = keep.tile([P, ROWS], U8, align_bytes=64)
        w_words = keep.tile([P, GATES * FEATURES * 2], U8, align_bytes=64)
        w_scales = keep.tile([P, GATES * FEATURES], U8, align_bytes=64)
        bias_row = keep.tile([P, GATES * FEATURES], BF16)
        ones = keep.tile([P, P], BF16)
        bias_cols = keep.tile([P, GATES * HALVES], F32)
        bias_wide = keep.tile([P, GATES * FEATURES], BF16)
        identity = keep.tile([P, P], F32)
        table_warmer = keep.tile([P, 2], F32)

        def tiles_of(j):
            return slice(j * PAIR, (j + 1) * PAIR)

        def load_x(j):
            nc.sync.dma_start(out=x_sb[:, tiles_of(j), :], in_=x_rows[:, tiles_of(j), :])

        def load_weight(gate, words, scales):
            nc.sync.dma_start(
                out=w_words[:, gate * FEATURES * 2 : (gate + 1) * FEATURES * 2].bitcast(I32),
                in_=words.rearrange("g p b -> (g p) b").bitcast(I32),
            )
            scale_rows = scales.rearrange("g q n -> (g q) n")
            for quadrant in range(QUADRANTS):
                nc.sync.dma_start(
                    out=w_scales[
                        32 * quadrant : 32 * quadrant + 4, gate * FEATURES : (gate + 1) * FEATURES
                    ].bitcast(I32),
                    in_=scale_rows[4 * quadrant : 4 * quadrant + 4, :].bitcast(I32),
                )

        def load_bias(gate, bias):
            nc.sync.dma_start(
                out=bias_row[0:1, gate * FEATURES : (gate + 1) * FEATURES], in_=bias.rearrange("(a n) -> a n", a=1)
            )

        turned = {}
        grouped = {}

        def turn_tile(t, target):
            words = x_sb[:, t, :].bitcast(F32)
            for parity in range(2):
                nc.tensor.transpose(target[:, parity, :], words[:, parity:WORDS:2], identity[:])

        def turn(j):
            if j < PAIRS:
                x_t = psum.tile([P, PAIR, 2, P], F32, tag="x_t")
                for i in range(PAIR):
                    turn_tile(j * PAIR + i, x_t[:, i])
                turned[j] = x_t

        def group(j, copy):
            if j < PAIRS:
                words = stage.tile([P, PAIR_ROWS * 4], BF16, align_bytes=64)
                grouped[j] = words
                copy(
                    out=words[:].bitcast(F32).rearrange("p (i r w) -> p i r w", i=PAIR, w=2),
                    in_=turned[j][:].rearrange("p i w r -> p i r w"),
                )

        def quantise_rows(first_row, rows, source):
            nc.vector.quantize_mx(
                out=x_codes[:, first_row : first_row + rows].bitcast(FP8X4),
                scales=x_scales[:, first_row : first_row + rows],
                in_=source,
            )

        def quantise(j):
            if j < PAIRS:
                quantise_rows(j * PAIR_ROWS, PAIR_ROWS, grouped[j][:])

        def first_pair():
            both = stage.tile([P, PAIR_ROWS * 4], BF16, align_bytes=64)
            for i, copy in enumerate((nc.scalar.copy, nc.vector.tensor_copy)):
                x_t = psum.tile([P, 2, P], F32, tag="out_t")
                turn_tile(i, x_t)
                copy(
                    out=both[:, i * P * 4 : (i + 1) * P * 4].bitcast(F32).rearrange("p (r w) -> p r w", w=2),
                    in_=x_t[:].rearrange("p w r -> p r w"),
                )
            for i in range(PAIR):
                quantise_rows(i * P, P, both[:, i * P * 4 : (i + 1) * P * 4])

        sums = {}

        def multiply_by_feature(j, gate):
            cols = slice(j * PAIR_ROWS, (j + 1) * PAIR_ROWS)
            bank = acc_pool.tile([P, HALVES, PAIR_ROWS], F32, tag="acc")
            for half in range(HALVES):
                block = gate * HALVES + half
                nc.tensor.matmul_mx(
                    out=bank[:, half, :],
                    lhsT=w_words[:, block * P * 2 : (block + 1) * P * 2].bitcast(FP4X4),
                    lhsT_scale=w_scales[:, block * P : (block + 1) * P],
                    rhs=x_codes[:, cols].bitcast(FP8X4),
                    rhs_scale=x_scales[:, cols],
                    start=True,
                    stop=True,
                )
            sums[j, gate] = bank

        def multiply_by_row(t, target, first_col, cols):
            rows = slice(t * P, (t + 1) * P)
            nc.tensor.matmul_mx(
                out=target,
                lhsT=x_codes[:, rows].bitcast(FP8X4),
                lhsT_scale=x_scales[:, rows],
                rhs=w_words[:, first_col * 2 : (first_col + cols) * 2].bitcast(FP4X4),
                rhs_scale=w_scales[:, first_col : first_col + cols],
                start=True,
                stop=True,
            )

        def multiply(j):
            if WAYS[j] == "X":
                for i in range(PAIR):
                    bank = acc_pool.tile([P, GATES * FEATURES], F32, tag="acc")
                    multiply_by_row(j * PAIR + i, bank[:], 0, GATES * FEATURES)
                    sums[j, i] = bank
                return
            multiply_by_feature(j, C)
            if WAYS[j] == "W":
                multiply_by_feature(j, O)
            else:
                bank = acc_pool.tile([P, PAIR, FEATURES], F32, tag="acc")
                for i in range(PAIR):
                    multiply_by_row(j * PAIR + i, bank[:, i, :], O * FEATURES, FEATURES)
                sums[j, O] = bank

        biased = {}
        sig_o = {}
        to_turn = {}

        def add_bias(j):
            if WAYS[j] == "M":
                biased_o = gates.tile([P, PAIR, FEATURES], F32)
                biased[j] = biased_o
                nc.vector.tensor_tensor(
                    out=biased_o[:],
                    in0=sums[j, O][:],
                    in1=bias_wide[:, O * FEATURES : (O + 1) * FEATURES].unsqueeze(1).to_broadcast([P, PAIR, FEATURES]),
                    op=ADD,
                )
            if WAYS[j] == "X":
                biased_both = gates.tile([P, PAIR, GATES * FEATURES], F32)
                biased[j] = biased_both
                for i in range(PAIR):
                    nc.vector.tensor_tensor(out=biased_both[:, i, :], in0=sums[j, i][:], in1=bias_wide[:], op=ADD)

        def sigmoid_by_feature(j, gate, half, result):
            block = gate * HALVES + half
            nc.scalar.activation(
                out=result[:, half, :], in_=sums[j, gate][:, half, :], func=SIGMOID, bias=bias_cols[:, block : block + 1]
            )

        def cell(j):
            c_sig = gates.tile([P, HALVES, PAIR_ROWS], F32)
            c_tanh = gates.tile([P, HALVES, PAIR_ROWS], F32)
            sigmoid_by_feature(j, C, 0, c_sig)
            sigmoid_by_feature(j, C, 1, c_sig)
            if WAYS[j] == "M":
                for half in range(HALVES):
                    nc.scalar.activation(out=c_tanh[:, half, :], in_=c_sig[:, half, :], func=TANH)
                to_turn[j] = c_tanh
                return
            o_sig = gates.tile([P, HALVES, PAIR_ROWS], F32)
            product = gates.tile([P, HALVES, PAIR_ROWS], F32)
            sigmoid_by_feature(j, O, 0, o_sig)
            nc.scalar.activation(out=c_tanh[:], in_=c_sig[:], func=TANH)
            for half in range(HALVES):
                if half == 1:
                    sigmoid_by_feature(j, O, 1, o_sig)
                nc.gpsimd.tensor_tensor(
                    out=product[:, half, :], in0=o_sig[:, half, :], in1=c_tanh[:, half, :], op=MULT
                )
            to_turn[j] = product

        def o_by_row(j):
            o_rows = gates.tile([P, PAIR, FEATURES], F32)
            sig_o[j] = o_rows
            nc.scalar.activation(out=o_rows[:], in_=biased[j][:], func=SIGMOID)

        def store(tiles, cols):
            nc.sync.dma_start(out=out_rows[:, tiles, cols], in_=out_sb[:, tiles, cols])

        def back(j):
            if j < 0:
                return
            out_t = psum.tile([P, PAIR, FEATURES], F32, tag="out_t")
            for i in range(PAIR):
                for half in range(HALVES):
                    nc.tensor.transpose(
                        out_t[:, i, half * P : (half + 1) * P], to_turn[j][:, half, i * P : (i + 1) * P], identity[:]
                    )
            if WAYS[j] == "M":
                nc.vector.tensor_tensor(out=out_sb[:, tiles_of(j), :], in0=out_t[:], in1=sig_o[j][:], op=MULT)
            else:
                nc.vector.tensor_copy(out=out_sb[:, tiles_of(j), :], in_=out_t[:])
            store(tiles_of(j), slice(0, FEATURES))

        def last_pair(j):
            sig = gates.tile([P, PAIR, GATES * FEATURES], F32)
            x_tanh = gates.tile([P, PAIR, FEATURES], F32)
            for i in range(PAIR):
                nc.scalar.activation(out=sig[:, i, :], in_=biased[j][:, i, :], func=SIGMOID)
            for i in range(PAIR):
                t = j * PAIR + i
                pieces = i + 1
                width = FEATURES // pieces
                for piece in range(pieces):
                    cols = slice(piece * width, (piece + 1) * width)
                    c_cols = slice(C * FEATURES + piece * width, C * FEATURES + (piece + 1) * width)
                    nc.scalar.activation(out=x_tanh[:, i, cols], in_=sig[:, i, c_cols], func=TANH)
                    nc.vector.tensor_tensor(
                        out=out_sb[:, t, cols], in0=sig[:, i, cols], in1=x_tanh[:, i, cols], op=MULT
                    )
                    store(slice(t, t + 1), cols)

        nc.gpsimd.memset(ones[:], 1.0)
        nc.vector.memset(table_warmer[:], 0.0)
        nc.vector.memset(w_scales[:].bitcast(I32), 0)
        nc.vector.memset(bias_row[:].bitcast(I32), 0)
        make_identity(nc, identity[:])
        warm_ps = acc_pool.tile([P, BANK], F32, tag="acc")
        for i in range(WARM_UPS):
            nc.tensor.matmul(out=warm_ps[:, 0:P], lhsT=ones[:], rhs=ones[:], start=True, stop=True)
        nc.scalar.activation(out=table_warmer[:, 1:2], in_=table_warmer[:, 0:1], func=SIGMOID)
        load_x(0)
        load_x(1)
        load_weight(C, wc_words, wc_scales)
        load_x(2)
        load_bias(C, biasc)
        load_weight(O, wo_words, wo_scales)
        load_bias(O, biaso)
        for j in range(3, PAIRS):
            load_x(j)


        def bias_columns(gate):
            cols_ps = psum.tile([P, HALVES], F32, tag="out_t")
            for half in range(HALVES):
                block = gate * HALVES + half
                nc.tensor.matmul(
                    out=cols_ps[:, half : half + 1],
                    lhsT=bias_row[:, block * P : (block + 1) * P],
                    rhs=ones[:, 0:1],
                    start=True,
                    stop=True,
                )
            nc.vector.tensor_copy(out=bias_cols[:, gate * HALVES : (gate + 1) * HALVES], in_=cols_ps[:])

        first_pair()
        turn(1)
        group(1, nc.scalar.copy)
        turn(2)
        bias_columns(C)
        multiply_by_feature(0, C)
        quantise(1)
        group(2, nc.vector.tensor_copy)
        multiply_by_feature(0, O)
        bias_columns(O)
        cell(0)
        quantise(2)
        multiply(1)
        wide_ps = psum.tile([P, GATES * FEATURES], BF16, tag="out_t")
        nc.tensor.matmul(out=wide_ps[:], lhsT=ones[:], rhs=bias_row[:], start=True, stop=True)
        nc.vector.tensor_copy(out=bias_wide[:], in_=wide_ps[:])
        turn(3)
        turn(4)
        for j in range(0, PAIRS - 2, 2):
            group(j + 3, nc.vector.tensor_copy)
            add_bias(j + 1)
            cell(j + 1)
            group(j + 4, nc.vector.tensor_copy)
            quantise(j + 3)
            quantise(j + 4)
            multiply(j + 2)
            add_bias(j + 2)
            cell(j + 2)
            o_by_row(j + 1)
            turn(j + 5)
            back(j - 1)
            back(j)
            turn(j + 6)
            multiply(j + 3)
        o_by_row(PAIRS - 2)
        add_bias(PAIRS - 1)
        back(PAIRS - 3)
        back(PAIRS - 2)
        last_pair(PAIRS - 1)
